import numpy as np
import ml_dtypes


def mxq(x, axis, fmt="e4m3"):
    dtype, down = {"e4m3": (ml_dtypes.float8_e4m3fn, 7), "e5m2": (ml_dtypes.float8_e5m2, 14)}[fmt]
    v = np.moveaxis(np.asarray(x, np.float32).astype(ml_dtypes.bfloat16).astype(np.float64), axis, -1)
    blocks = v.reshape(v.shape[:-1] + (-1, 32))
    amax = np.abs(blocks).max(-1, keepdims=True)
    byte = np.maximum(np.where(amax > 0, np.frexp(amax)[1] - 1 + 127, 0) - down, 1)
    scale = np.exp2(byte - 127.0)
    codes = (blocks / scale).astype(np.float32).astype(dtype).astype(np.float64)
    return np.moveaxis((codes * scale).reshape(v.shape), -1, axis)


WIDE = False


def mx_kscale(k):
    if not WIDE:
        return np.ones(k)
    levels = np.array([10, -10, 5, -5, 0])
    a = np.random.permutation(np.resize(levels, k // 512 * 4)).reshape(k // 512, 4)
    idx = np.arange(k)
    return np.exp2(a[idx // 512, idx % 128 // 32])


BF16 = ml_dtypes.bfloat16


def bf(x):
    return np.asarray(x, np.float32).astype(BF16)


def f64(x):
    return np.asarray(x).astype(np.float64)


B, T, C, H, QB = 4, 1024, 1024, 128, 512
GAMMA = 0.96875


def decay(n0, n1, m1):
    dist = np.arange(n0, n1)[:, None] - np.arange(m1)[None, :]
    return np.where(dist >= 0, GAMMA ** f64(np.maximum(dist, 0)), 0.0)


def setup_inputs():
    s, f = mx_kscale(C), mx_kscale(T)
    return {"q": bf(np.random.standard_normal((B, T, H))),
            "k": bf(np.random.standard_normal((B, T, H)) * f[:, None]),
            "x": bf(np.random.standard_normal((B, T, C)) * s / f[:, None]),
            "Wv": bf(np.random.standard_normal((C, H)) / np.sqrt(C) / s[:, None])}


def reference(q, k, x, Wv):
    q, k = f64(q), f64(k)
    v = mxq(f64(x), 2, "e4m3") @ mxq(f64(Wv), 0, "e4m3")
    vq = mxq(v, 1, "e4m3")
    scale = C ** -0.5
    rows = []
    for n0 in range(0, T, QB):
        n1 = n0 + QB
        wei = q[:, n0:n1] @ k[:, :n1].transpose(0, 2, 1) * scale * decay(n0, n1, n1)
        rows.append(mxq(wei, 2, "e4m3") @ vq[:, :n1])
    return np.concatenate(rows, axis=1)

@@ -1,0 +1,222 @@
+import math
+
+import concourse.mybir as mybir
+from concourse.masks import make_identity
+
+F32 = mybir.dt.float32
+BF16 = mybir.dt.bfloat16
+U32 = mybir.dt.uint32
+U8 = mybir.dt.uint8
+FP8X4 = mybir.dt.float8_e4m3fn_x4
+
+B, T, C, H = 4, 1024, 1024, 128
+GAMMA = 0.96875
+SCALE = C**-0.5
+
+P = 128
+PACK = 4
+K_PASS = P * PACK
+GROUPS = T // K_PASS
+C_PASSES = C // K_PASS
+TILES = K_PASS // P
+
+BLOCKS = [(0, 0), (1, 0), (1, 1)]
+
+FLOPS = 2 * B * T * C * H + 2 * 2 * B * len(BLOCKS) * K_PASS * K_PASS * H
+
+
+def tile_retentionhead_pa_kernel(tc, q, k, x, Wv, out):
+    nc = tc.nc
+    with (
+        tc.tile_pool(name="loads", bufs=1) as loads,
+        tc.tile_pool(name="const", bufs=1) as const,
+        tc.tile_pool(name="work", bufs=2) as work,
+        tc.psum_pool(name="psum", bufs=1) as psum,
+    ):
+        wv_sb = loads.tile([P, C_PASSES * PACK, H], BF16)
+        nc.sync.dma_start(
+            out=wv_sb[:].rearrange("w (a e) h -> w a (e h)", e=2),
+            in_=Wv.rearrange("(a w e) h -> w a (e h)", w=P, e=2),
+        )
+        q_sb, k_sb, x_sb = [], [], []
+        for b in range(B):
+            q_tile = loads.tile([P, T // P, H], BF16, name="q%d" % b)
+            nc.sync.dma_start(out=q_tile[:], in_=q[b].rearrange("(r p) h -> p r h", p=P))
+            q_sb.append(q_tile)
+            k_tile = loads.tile([P, GROUPS, PACK, H], BF16, name="k%d" % b)
+            nc.sync.dma_start(
+                out=k_tile[:].rearrange("p g t h -> p g (t h)"),
+                in_=k[b].rearrange("(g p t) h -> p g (t h)", p=P, t=PACK),
+            )
+            k_sb.append(k_tile)
+            for g in range(GROUPS):
+                x_tile = loads.tile([P, PACK * C], BF16, name="x%d_%d" % (b, g))
+                rows = x[b, g * K_PASS : (g + 1) * K_PASS, :]
+                nc.sync.dma_start(out=x_tile[:], in_=rows.rearrange("(p t) c -> p (t c)", t=PACK))
+                x_sb.append(x_tile)
+
+        ident_bf16 = const.tile([P, P], BF16)
+        make_identity(nc, ident_bf16[:])
+        ident_f32 = const.tile([P, P], F32)
+        make_identity(nc, ident_f32[:])
+
+        dist = const.tile([P, P, PACK], F32)
+        nc.gpsimd.iota(
+            dist[:],
+            pattern=[[1, P], [-1, PACK]],
+            base=0,
+            channel_multiplier=-PACK,
+            allow_small_or_imprecise_dtypes=True,
+        )
+        decay = const.tile([P, P, PACK], F32)
+        nc.scalar.activation(
+            out=decay[:], in_=dist[:], func=mybir.ActivationFunctionType.Exp, scale=math.log(GAMMA)
+        )
+        near = const.tile([P, K_PASS, PACK], F32)
+        far = const.tile([P, K_PASS, PACK], F32)
+        for j in range(TILES):
+            cols = slice(j * P, (j + 1) * P)
+            nc.vector.tensor_scalar_mul(out=near[:, cols, :], in0=decay[:], scalar1=SCALE * GAMMA ** (j * P))
+            nc.vector.tensor_scalar_mul(
+                out=far[:, cols, :], in0=decay[:], scalar1=SCALE * GAMMA ** (K_PASS + j * P)
+            )
+        nc.gpsimd.affine_select(
+            out=near[:],
+            in_=near[:],
+            pattern=[[1, K_PASS], [-1, PACK]],
+            compare_op=mybir.AluOpType.is_ge,
+            fill=0.0,
+            base=0,
+            channel_multiplier=-PACK,
+        )
+
+        wv_grouped = const.tile([P, C_PASSES, H, PACK], BF16, align_bytes=64)
+        for G in range(C_PASSES):
+            nc.vector.tensor_copy(
+                out=wv_grouped[:, G],
+                in_=wv_sb[:, G * PACK : (G + 1) * PACK, :].rearrange("w s h -> w h s"),
+            )
+        wv_codes = const.tile([P, C_PASSES * H], U32, align_bytes=64)
+        wv_scales = const.tile([P, C_PASSES * H], U8, align_bytes=64)
+        nc.vector.quantize_mx(
+            out=wv_codes[:].bitcast(FP8X4),
+            scales=wv_scales[:],
+            in_=wv_grouped[:].rearrange("w G h s -> w (G h s)"),
+        )
+
+        def transpose_q_and_k(b):
+            qT_ps = psum.tile([P, T], BF16, tag="qk_ps")
+            for r in range(T // P):
+                nc.tensor.transpose(qT_ps[:, r * P : (r + 1) * P], q_sb[b][:, r, :], ident_bf16[:])
+            qT = work.tile([P, T], BF16, tag="qT")
+            nc.scalar.copy(out=qT[:], in_=qT_ps[:])
+            kT_ps = psum.tile([P, T], BF16, tag="qk_ps")
+            for g in range(GROUPS):
+                for t in range(PACK):
+                    col = (g * PACK + t) * P
+                    nc.tensor.transpose(kT_ps[:, col : col + P], k_sb[b][:, g, t, :], ident_bf16[:])
+            kT = work.tile([P, T], BF16, tag="kT")
+            nc.scalar.copy(out=kT[:], in_=kT_ps[:])
+            return qT, kT
+
+        def project(b, g):
+            x_words = x_sb[b * GROUPS + g][:].bitcast(F32)
+            words_per_row = C // 2
+            x_grouped = work.tile([P, PACK * C], BF16, tag="x_grouped", align_bytes=64)
+            x_codes = work.tile([P, C], U32, tag="x_codes", align_bytes=64)
+            x_scales = work.tile([P, C], U8, tag="x_scales", align_bytes=64)
+            for t in range(PACK):
+                xT = psum.tile([P, C_PASSES, 2, P], F32, tag="xT", bufs=2)
+                for G in range(C_PASSES):
+                    for u in range(2):
+                        col = t * words_per_row + (G * 2 + u) * P
+                        nc.tensor.transpose(xT[:, G, u, :], x_words[:, col : col + P], ident_f32[:])
+                nc.scalar.copy(
+                    out=x_grouped[:]
+                    .bitcast(F32)[:, t * words_per_row : (t + 1) * words_per_row]
+                    .rearrange("w (G p u) -> w G p u", G=C_PASSES, u=2),
+                    in_=xT[:].rearrange("w G u p -> w G p u"),
+                )
+                nc.vector.quantize_mx(
+                    out=x_codes[:, t * C_PASSES * P : (t + 1) * C_PASSES * P].bitcast(FP8X4),
+                    scales=x_scales[:, t * C_PASSES * P : (t + 1) * C_PASSES * P],
+                    in_=x_grouped[:, t * C : (t + 1) * C],
+                )
+            v_ps = psum.tile([P, PACK, H], F32, tag="v_ps")
+            for t in range(PACK):
+                for G in range(C_PASSES):
+                    rows = slice((t * C_PASSES + G) * P, (t * C_PASSES + G + 1) * P)
+                    nc.tensor.matmul_mx(
+                        out=v_ps[:, t, :],
+                        lhsT=x_codes[:, rows].bitcast(FP8X4),
+                        lhsT_scale=x_scales[:, rows],
+                        rhs=wv_codes[:, G * H : (G + 1) * H].bitcast(FP8X4),
+                        rhs_scale=wv_scales[:, G * H : (G + 1) * H],
+                        start=(G == 0),
+                        stop=(G == C_PASSES - 1),
+                    )
+            v_grouped = work.tile([P, H, PACK], BF16, tag="v_grouped", align_bytes=64)
+            nc.scalar.copy(out=v_grouped[:], in_=v_ps[:].rearrange("p t h -> p h t"))
+            v_codes = work.tile([P, H], U32, tag="v_codes", bufs=4, align_bytes=64)
+            v_scales = work.tile([P, H], U8, tag="v_scales", bufs=4, align_bytes=64)
+            nc.vector.quantize_mx(
+                out=v_codes[:].bitcast(FP8X4),
+                scales=v_scales[:],
+                in_=v_grouped[:].rearrange("p h t -> p (h t)"),
+            )
+            return v_codes, v_scales
+
+        def weigh(qT, kT, block, g):
+            table = near if block == g else far
+            w_grouped = work.tile([P, K_PASS, PACK], BF16, tag="w_grouped", bufs=3, align_bytes=64)
+            for j in range(TILES):
+                queries = slice(block * K_PASS + j * P, block * K_PASS + (j + 1) * P)
+                s_ps = psum.tile([P, PACK, P], F32, tag="s_ps", bufs=3)
+                for t in range(PACK):
+                    col = (g * PACK + t) * P
+                    nc.tensor.matmul(
+                        out=s_ps[:, t, :], lhsT=kT[:, col : col + P], rhs=qT[:, queries], start=True, stop=True
+                    )
+                nc.vector.tensor_tensor(
+                    out=w_grouped[:, j * P : (j + 1) * P, :],
+                    in0=s_ps[:].rearrange("p t c -> p c t"),
+                    in1=table[:, j * P : (j + 1) * P, :],
+                    op=mybir.AluOpType.mult,
+                )
+            w_codes = work.tile([P, K_PASS], U32, tag="w_codes", bufs=6, align_bytes=64)
+            w_scales = work.tile([P, K_PASS], U8, tag="w_scales", bufs=6, align_bytes=64)
+            nc.vector.quantize_mx(
+                out=w_codes[:].bitcast(FP8X4),
+                scales=w_scales[:],
+                in_=w_grouped[:].rearrange("p c t -> p (c t)"),
+            )
+            return w_codes, w_scales
+
+        def retain(b, block, w_mx, v_mx):
+            o_ps = psum.tile([P, TILES, H], F32, tag="o_ps")
+            for j in range(TILES):
+                for g in range(block + 1):
+                    w_codes, w_scales = w_mx[(block, g)]
+                    v_codes, v_scales = v_mx[g]
+                    nc.tensor.matmul_mx(
+                        out=o_ps[:, j, :],
+                        lhsT=w_codes[:, j * P : (j + 1) * P].bitcast(FP8X4),
+                        lhsT_scale=w_scales[:, j * P : (j + 1) * P],
+                        rhs=v_codes[:].bitcast(FP8X4),
+                        rhs_scale=v_scales[:],
+                        start=(g == 0),
+                        stop=(g == block),
+                    )
+            o_sb = work.tile([P, TILES, H], F32, tag="o_sb", bufs=3)
+            nc.scalar.copy(out=o_sb[:], in_=o_ps[:])
+            rows = out[b, block * K_PASS : (block + 1) * K_PASS, :]
+            nc.sync.dma_start(out=rows.rearrange("(j p) h -> p j h", p=P), in_=o_sb[:])
+
+        for b in range(B):
+            qT, kT = transpose_q_and_k(b)
+            v_mx = [project(b, g) for g in range(GROUPS)]
+            w_mx = {}
+            for block, g in BLOCKS:
+                w_mx[(block, g)] = weigh(qT, kT, block, g)
+            for block in range(GROUPS):
+                retain(b, block, w_mx, v_mx)

@@ -22,6 +22,8 @@ TILES = K_PASS // P
 
 BLOCKS = [(0, 0), (1, 0), (1, 1)]
 
+MX_STEP = 2
+
 FLOPS = 2 * B * T * C * H + 2 * 2 * B * len(BLOCKS) * K_PASS * K_PASS * H
 
 
@@ -32,12 +34,9 @@ def tile_retentionhead_pa_kernel(tc, q, k, x, Wv, out):
         tc.tile_pool(name="const", bufs=1) as const,
         tc.tile_pool(name="work", bufs=2) as work,
         tc.psum_pool(name="psum", bufs=1) as psum,
+        tc.manual_schedule(),
     ):
         wv_sb = loads.tile([P, C_PASSES * PACK, H], BF16)
-        nc.sync.dma_start(
-            out=wv_sb[:].rearrange("w (a e) h -> w a (e h)", e=2),
-            in_=Wv.rearrange("(a w e) h -> w a (e h)", w=P, e=2),
-        )
         q_sb, k_sb, x_sb = [], [], []
         for b in range(B):
             q_tile = loads.tile([P, T // P, H], BF16, name="q%d" % b)
@@ -51,9 +50,14 @@ def tile_retentionhead_pa_kernel(tc, q, k, x, Wv, out):
             k_sb.append(k_tile)
             for g in range(GROUPS):
                 x_tile = loads.tile([P, PACK * C], BF16, name="x%d_%d" % (b, g))
-                rows = x[b, g * K_PASS : (g + 1) * K_PASS, :]
-                nc.sync.dma_start(out=x_tile[:], in_=rows.rearrange("(p t) c -> p (t c)", t=PACK))
+                x_rows = x[b, g * K_PASS : (g + 1) * K_PASS, :]
+                nc.sync.dma_start(out=x_tile[:], in_=x_rows.rearrange("(p t) c -> p (t c)", t=PACK))
                 x_sb.append(x_tile)
+                if b == 0 and g == 0:
+                    nc.sync.dma_start(
+                        out=wv_sb[:].rearrange("w (a e) h -> w a (e h)", e=2),
+                        in_=Wv.rearrange("(a w e) h -> w a (e h)", w=P, e=2),
+                    )
 
         ident_bf16 = const.tile([P, P], BF16)
         make_identity(nc, ident_bf16[:])
@@ -77,79 +81,74 @@ def tile_retentionhead_pa_kernel(tc, q, k, x, Wv, out):
         for j in range(TILES):
             cols = slice(j * P, (j + 1) * P)
             nc.vector.tensor_scalar_mul(out=near[:, cols, :], in0=decay[:], scalar1=SCALE * GAMMA ** (j * P))
-            nc.vector.tensor_scalar_mul(
-                out=far[:, cols, :], in0=decay[:], scalar1=SCALE * GAMMA ** (K_PASS + j * P)
+            nc.gpsimd.affine_select(
+                out=near[:, cols, :],
+                in_=near[:, cols, :],
+                pattern=[[1, P], [-1, PACK]],
+                compare_op=mybir.AluOpType.is_ge,
+                fill=0.0,
+                base=j * P,
+                channel_multiplier=-PACK,
             )
-        nc.gpsimd.affine_select(
-            out=near[:],
-            in_=near[:],
-            pattern=[[1, K_PASS], [-1, PACK]],
-            compare_op=mybir.AluOpType.is_ge,
-            fill=0.0,
-            base=0,
-            channel_multiplier=-PACK,
-        )
+
+        def transpose_q_or_k(tiles_of_128_rows, name):
+            rows_ps = psum.tile([P, T], BF16, tag="qk_ps")
+            for r in range(T // P):
+                nc.tensor.transpose(rows_ps[:, r * P : (r + 1) * P], tiles_of_128_rows[:, r, :], ident_bf16[:])
+            rows_T = work.tile([P, T], BF16, tag=name, name=name)
+            nc.scalar.copy(out=rows_T[:], in_=rows_ps[:])
+            return rows_T
+
+        def transpose_q(b):
+            return transpose_q_or_k(q_sb[b][:], "qT")
+
+        def transpose_k(b):
+            return transpose_q_or_k(k_sb[b][:].rearrange("p g t h -> p (g t) h"), "kT")
+
+        qT = transpose_q(0)
+        kT = transpose_k(0)
 
         wv_grouped = const.tile([P, C_PASSES, H, PACK], BF16, align_bytes=64)
-        for G in range(C_PASSES):
-            nc.vector.tensor_copy(
-                out=wv_grouped[:, G],
-                in_=wv_sb[:, G * PACK : (G + 1) * PACK, :].rearrange("w s h -> w h s"),
-            )
         wv_codes = const.tile([P, C_PASSES * H], U32, align_bytes=64)
         wv_scales = const.tile([P, C_PASSES * H], U8, align_bytes=64)
-        nc.vector.quantize_mx(
-            out=wv_codes[:].bitcast(FP8X4),
-            scales=wv_scales[:],
-            in_=wv_grouped[:].rearrange("w G h s -> w (G h s)"),
-        )
 
-        def transpose_q_and_k(b):
-            qT_ps = psum.tile([P, T], BF16, tag="qk_ps")
-            for r in range(T // P):
-                nc.tensor.transpose(qT_ps[:, r * P : (r + 1) * P], q_sb[b][:, r, :], ident_bf16[:])
-            qT = work.tile([P, T], BF16, tag="qT")
-            nc.scalar.copy(out=qT[:], in_=qT_ps[:])
-            kT_ps = psum.tile([P, T], BF16, tag="qk_ps")
-            for g in range(GROUPS):
-                for t in range(PACK):
-                    col = (g * PACK + t) * P
-                    nc.tensor.transpose(kT_ps[:, col : col + P], k_sb[b][:, g, t, :], ident_bf16[:])
-            kT = work.tile([P, T], BF16, tag="kT")
-            nc.scalar.copy(out=kT[:], in_=kT_ps[:])
-            return qT, kT
+        def quantise_wv():
+            for G in range(C_PASSES):
+                nc.vector.tensor_copy(
+                    out=wv_grouped[:, G],
+                    in_=wv_sb[:, G * PACK : (G + 1) * PACK, :].rearrange("w s h -> w h s"),
+                )
+            nc.vector.quantize_mx(
+                out=wv_codes[:].bitcast(FP8X4),
+                scales=wv_scales[:],
+                in_=wv_grouped[:].rearrange("w G h s -> w (G h s)"),
+            )
 
-        def project(b, g):
+        words_per_row = C // 2
+
+        def transpose_x(b, g, t, x_grouped):
             x_words = x_sb[b * GROUPS + g][:].bitcast(F32)
-            words_per_row = C // 2
-            x_grouped = work.tile([P, PACK * C], BF16, tag="x_grouped", align_bytes=64)
-            x_codes = work.tile([P, C], U32, tag="x_codes", align_bytes=64)
-            x_scales = work.tile([P, C], U8, tag="x_scales", align_bytes=64)
-            for t in range(PACK):
-                xT = psum.tile([P, C_PASSES, 2, P], F32, tag="xT", bufs=2)
-                for G in range(C_PASSES):
-                    for u in range(2):
-                        col = t * words_per_row + (G * 2 + u) * P
-                        nc.tensor.transpose(xT[:, G, u, :], x_words[:, col : col + P], ident_f32[:])
-                nc.scalar.copy(
-                    out=x_grouped[:]
-                    .bitcast(F32)[:, t * words_per_row : (t + 1) * words_per_row]
-                    .rearrange("w (G p u) -> w G p u", G=C_PASSES, u=2),
-                    in_=xT[:].rearrange("w G u p -> w G p u"),
-                )
-                nc.vector.quantize_mx(
-                    out=x_codes[:, t * C_PASSES * P : (t + 1) * C_PASSES * P].bitcast(FP8X4),
-                    scales=x_scales[:, t * C_PASSES * P : (t + 1) * C_PASSES * P],
-                    in_=x_grouped[:, t * C : (t + 1) * C],
-                )
+            xT = psum.tile([P, C_PASSES, 2, P], F32, tag="xT", bufs=2)
+            for G in range(C_PASSES):
+                for u in range(2):
+                    col = t * words_per_row + (G * 2 + u) * P
+                    nc.tensor.transpose(xT[:, G, u, :], x_words[:, col : col + P], ident_f32[:])
+            nc.scalar.copy(
+                out=x_grouped[:]
+                .bitcast(F32)[:, t * words_per_row : (t + 1) * words_per_row]
+                .rearrange("w (G p u) -> w G p u", G=C_PASSES, u=2),
+                in_=xT[:].rearrange("w G u p -> w G p u"),
+            )
+
+        def project(x_codes, x_scales):
             v_ps = psum.tile([P, PACK, H], F32, tag="v_ps")
             for t in range(PACK):
                 for G in range(C_PASSES):
-                    rows = slice((t * C_PASSES + G) * P, (t * C_PASSES + G + 1) * P)
+                    cols = slice((t * C_PASSES + G) * P, (t * C_PASSES + G + 1) * P)
                     nc.tensor.matmul_mx(
                         out=v_ps[:, t, :],
-                        lhsT=x_codes[:, rows].bitcast(FP8X4),
-                        lhsT_scale=x_scales[:, rows],
+                        lhsT=x_codes[:, cols].bitcast(FP8X4),
+                        lhsT_scale=x_scales[:, cols],
                         rhs=wv_codes[:, G * H : (G + 1) * H].bitcast(FP8X4),
                         rhs_scale=wv_scales[:, G * H : (G + 1) * H],
                         start=(G == 0),
@@ -157,40 +156,7 @@ def tile_retentionhead_pa_kernel(tc, q, k, x, Wv, out):
                     )
             v_grouped = work.tile([P, H, PACK], BF16, tag="v_grouped", align_bytes=64)
             nc.scalar.copy(out=v_grouped[:], in_=v_ps[:].rearrange("p t h -> p h t"))
-            v_codes = work.tile([P, H], U32, tag="v_codes", bufs=4, align_bytes=64)
-            v_scales = work.tile([P, H], U8, tag="v_scales", bufs=4, align_bytes=64)
-            nc.vector.quantize_mx(
-                out=v_codes[:].bitcast(FP8X4),
-                scales=v_scales[:],
-                in_=v_grouped[:].rearrange("p h t -> p (h t)"),
-            )
-            return v_codes, v_scales
-
-        def weigh(qT, kT, block, g):
-            table = near if block == g else far
-            w_grouped = work.tile([P, K_PASS, PACK], BF16, tag="w_grouped", bufs=3, align_bytes=64)
-            for j in range(TILES):
-                queries = slice(block * K_PASS + j * P, block * K_PASS + (j + 1) * P)
-                s_ps = psum.tile([P, PACK, P], F32, tag="s_ps", bufs=3)
-                for t in range(PACK):
-                    col = (g * PACK + t) * P
-                    nc.tensor.matmul(
-                        out=s_ps[:, t, :], lhsT=kT[:, col : col + P], rhs=qT[:, queries], start=True, stop=True
-                    )
-                nc.vector.tensor_tensor(
-                    out=w_grouped[:, j * P : (j + 1) * P, :],
-                    in0=s_ps[:].rearrange("p t c -> p c t"),
-                    in1=table[:, j * P : (j + 1) * P, :],
-                    op=mybir.AluOpType.mult,
-                )
-            w_codes = work.tile([P, K_PASS], U32, tag="w_codes", bufs=6, align_bytes=64)
-            w_scales = work.tile([P, K_PASS], U8, tag="w_scales", bufs=6, align_bytes=64)
-            nc.vector.quantize_mx(
-                out=w_codes[:].bitcast(FP8X4),
-                scales=w_scales[:],
-                in_=w_grouped[:].rearrange("p c t -> p (c t)"),
-            )
-            return w_codes, w_scales
+            return v_grouped
 
         def retain(b, block, w_mx, v_mx):
             o_ps = psum.tile([P, TILES, H], F32, tag="o_ps")
@@ -209,14 +175,84 @@ def tile_retentionhead_pa_kernel(tc, q, k, x, Wv, out):
                     )
             o_sb = work.tile([P, TILES, H], F32, tag="o_sb", bufs=3)
             nc.scalar.copy(out=o_sb[:], in_=o_ps[:])
-            rows = out[b, block * K_PASS : (block + 1) * K_PASS, :]
-            nc.sync.dma_start(out=rows.rearrange("(j p) h -> p j h", p=P), in_=o_sb[:])
+            out_rows = out[b, block * K_PASS : (block + 1) * K_PASS, :]
+            nc.sync.dma_start(out=out_rows.rearrange("(j p) h -> p j h", p=P), in_=o_sb[:])
 
+        v_mx, w_mx = {}, {}
+        old_v_mx, old_w_mx = {}, {}
+        x_mx = None
         for b in range(B):
-            qT, kT = transpose_q_and_k(b)
-            v_mx = [project(b, g) for g in range(GROUPS)]
-            w_mx = {}
-            for block, g in BLOCKS:
-                w_mx[(block, g)] = weigh(qT, kT, block, g)
-            for block in range(GROUPS):
-                retain(b, block, w_mx, v_mx)
+            for phase, (block, g) in enumerate(BLOCKS):
+                table = near if block == g else far
+                with_x = phase < GROUPS
+                v_grouped = None
+                w_grouped = work.tile([P, K_PASS, PACK], BF16, tag="w_grouped", bufs=2, align_bytes=64)
+                if with_x:
+                    x_grouped = work.tile([P, PACK * C], BF16, tag="x_grouped", align_bytes=64)
+                    x_codes = work.tile([P, C], U32, tag="x_codes", align_bytes=64)
+                    x_scales = work.tile([P, C], U8, tag="x_scales", align_bytes=64)
+                for j in range(TILES):
+                    queries = slice(block * K_PASS + j * P, block * K_PASS + (j + 1) * P)
+                    s_ps = psum.tile([P, PACK, P], F32, tag="s_ps", bufs=3)
+                    for t in range(PACK):
+                        col = (g * PACK + t) * P
+                        nc.tensor.matmul(
+                            out=s_ps[:, t, :], lhsT=kT[:, col : col + P], rhs=qT[:, queries], start=True, stop=True
+                        )
+                    if with_x:
+                        transpose_x(b, phase, j, x_grouped)
+                    if b == 0 and phase == 0:
+                        nc.scalar.mul(
+                            out=far[:, j * P : (j + 1) * P, :], in_=decay[:], mul=SCALE * GAMMA ** (K_PASS + j * P)
+                        )
+                    if phase == GROUPS and b + 1 < B and j == 0:
+                        next_qT = transpose_q(b + 1)
+                    if phase == GROUPS and b + 1 < B and j == 1:
+                        next_kT = transpose_k(b + 1)
+                    if j == MX_STEP:
+                        if phase == 0 and b > 0:
+                            retain(b - 1, 1, old_w_mx, old_v_mx)
+                        if phase == 1:
+                            v_grouped = project(x_mx[0], x_mx[1])
+                        if phase == 2:
+                            retain(b, 0, w_mx, v_mx)
+                            v_grouped = project(x_mx[0], x_mx[1])
+                    nc.vector.tensor_tensor(
+                        out=w_grouped[:, j * P : (j + 1) * P, :],
+                        in0=s_ps[:].rearrange("p t c -> p c t"),
+                        in1=table[:, j * P : (j + 1) * P, :],
+                        op=mybir.AluOpType.mult,
+                    )
+                    if with_x:
+                        cols = slice(j * C_PASSES * P, (j + 1) * C_PASSES * P)
+                        nc.vector.quantize_mx(
+                            out=x_codes[:, cols].bitcast(FP8X4),
+                            scales=x_scales[:, cols],
+                            in_=x_grouped[:, j * C : (j + 1) * C],
+                        )
+                if b == 0 and phase == 0:
+                    quantise_wv()
+                w_codes = work.tile([P, K_PASS], U32, tag="w_codes", bufs=6, align_bytes=64)
+                w_scales = work.tile([P, K_PASS], U8, tag="w_scales", bufs=6, align_bytes=64)
+                nc.vector.quantize_mx(
+                    out=w_codes[:].bitcast(FP8X4),
+                    scales=w_scales[:],
+                    in_=w_grouped[:].rearrange("p c t -> p (c t)"),
+                )
+                w_mx[(block, g)] = (w_codes, w_scales)
+                if v_grouped is not None:
+                    v_codes = work.tile([P, H], U32, tag="v_codes", bufs=4, align_bytes=64)
+                    v_scales = work.tile([P, H], U8, tag="v_scales", bufs=4, align_bytes=64)
+                    nc.vector.quantize_mx(
+                        out=v_codes[:].bitcast(FP8X4),
+                        scales=v_scales[:],
+                        in_=v_grouped[:].rearrange("p h t -> p (h t)"),
+                    )
+                    v_mx[phase - 1] = (v_codes, v_scales)
+                if with_x:
+                    x_mx = (x_codes, x_scales)
+            old_v_mx, old_w_mx = v_mx, w_mx
+            v_mx, w_mx = {}, {}
+            if b + 1 < B:
+                qT, kT = next_qT, next_kT
+        retain(B - 1, 1, old_w_mx, old_v_mx)

@@ -62,7 +62,7 @@ def tile_retentionhead_pa_kernel(tc, q, k, x, Wv, out):
         ident_bf16 = const.tile([P, P], BF16)
         make_identity(nc, ident_bf16[:])
         ident_f32 = const.tile([P, P], F32)
-        make_identity(nc, ident_f32[:])
+        nc.vector.tensor_copy(out=ident_f32[:], in_=ident_bf16[:])
 
         dist = const.tile([P, P, PACK], F32)
         nc.gpsimd.iota(
@@ -76,23 +76,21 @@ def tile_retentionhead_pa_kernel(tc, q, k, x, Wv, out):
         nc.scalar.activation(
             out=decay[:], in_=dist[:], func=mybir.ActivationFunctionType.Exp, scale=math.log(GAMMA)
         )
-        near = const.tile([P, K_PASS, PACK], F32)
-        far = const.tile([P, K_PASS, PACK], F32)
+        masked = []
         for j in range(TILES):
-            cols = slice(j * P, (j + 1) * P)
-            nc.vector.tensor_scalar_mul(out=near[:, cols, :], in0=decay[:], scalar1=SCALE * GAMMA ** (j * P))
-            nc.gpsimd.affine_select(
-                out=near[:, cols, :],
-                in_=near[:, cols, :],
-                pattern=[[1, P], [-1, PACK]],
-                compare_op=mybir.AluOpType.is_ge,
-                fill=0.0,
-                base=j * P,
-                channel_multiplier=-PACK,
+            masked_j = const.tile([P, P, PACK], F32, name="masked%d" % j)
+            nc.vector.scalar_tensor_tensor(
+                out=masked_j[:],
+                in0=dist[:],
+                scalar=float(-j * P),
+                in1=decay[:],
+                op0=mybir.AluOpType.is_ge,
+                op1=mybir.AluOpType.mult,
             )
+            masked.append(masked_j)
 
         def transpose_q_or_k(tiles_of_128_rows, name):
-            rows_ps = psum.tile([P, T], BF16, tag="qk_ps")
+            rows_ps = psum.tile([P, T], BF16, tag="transposed", bufs=2)
             for r in range(T // P):
                 nc.tensor.transpose(rows_ps[:, r * P : (r + 1) * P], tiles_of_128_rows[:, r, :], ident_bf16[:])
             rows_T = work.tile([P, T], BF16, tag=name, name=name)
@@ -128,7 +126,7 @@ def tile_retentionhead_pa_kernel(tc, q, k, x, Wv, out):
 
         def transpose_x(b, g, t, x_grouped):
             x_words = x_sb[b * GROUPS + g][:].bitcast(F32)
-            xT = psum.tile([P, C_PASSES, 2, P], F32, tag="xT", bufs=2)
+            xT = psum.tile([P, C_PASSES, 2, P], F32, tag="transposed", bufs=2)
             for G in range(C_PASSES):
                 for u in range(2):
                     col = t * words_per_row + (G * 2 + u) * P
@@ -183,7 +181,7 @@ def tile_retentionhead_pa_kernel(tc, q, k, x, Wv, out):
         x_mx = None
         for b in range(B):
             for phase, (block, g) in enumerate(BLOCKS):
-                table = near if block == g else far
+                gap = (block - g) * K_PASS
                 with_x = phase < GROUPS
                 v_grouped = None
                 w_grouped = work.tile([P, K_PASS, PACK], BF16, tag="w_grouped", bufs=2, align_bytes=64)
@@ -193,7 +191,7 @@ def tile_retentionhead_pa_kernel(tc, q, k, x, Wv, out):
                     x_scales = work.tile([P, C], U8, tag="x_scales", align_bytes=64)
                 for j in range(TILES):
                     queries = slice(block * K_PASS + j * P, block * K_PASS + (j + 1) * P)
-                    s_ps = psum.tile([P, PACK, P], F32, tag="s_ps", bufs=3)
+                    s_ps = psum.tile([P, PACK, P], F32, tag="s_ps", bufs=4)
                     for t in range(PACK):
                         col = (g * PACK + t) * P
                         nc.tensor.matmul(
@@ -201,10 +199,6 @@ def tile_retentionhead_pa_kernel(tc, q, k, x, Wv, out):
                         )
                     if with_x:
                         transpose_x(b, phase, j, x_grouped)
-                    if b == 0 and phase == 0:
-                        nc.scalar.mul(
-                            out=far[:, j * P : (j + 1) * P, :], in_=decay[:], mul=SCALE * GAMMA ** (K_PASS + j * P)
-                        )
                     if phase == GROUPS and b + 1 < B and j == 0:
                         next_qT = transpose_q(b + 1)
                     if phase == GROUPS and b + 1 < B and j == 1:
@@ -217,11 +211,13 @@ def tile_retentionhead_pa_kernel(tc, q, k, x, Wv, out):
                         if phase == 2:
                             retain(b, 0, w_mx, v_mx)
                             v_grouped = project(x_mx[0], x_mx[1])
-                    nc.vector.tensor_tensor(
+                    nc.vector.scalar_tensor_tensor(
                         out=w_grouped[:, j * P : (j + 1) * P, :],
                         in0=s_ps[:].rearrange("p t c -> p c t"),
-                        in1=table[:, j * P : (j + 1) * P, :],
-                        op=mybir.AluOpType.mult,
+                        scalar=SCALE * GAMMA ** (gap + j * P),
+                        in1=(masked[j] if gap == 0 else decay)[:],
+                        op0=mybir.AluOpType.mult,
+                        op1=mybir.AluOpType.mult,
                     )
                     if with_x:
                         cols = slice(j * C_PASSES * P, (j + 1) * C_PASSES * P)

@@ -22,8 +22,6 @@ TILES = K_PASS // P
 
 BLOCKS = [(0, 0), (1, 0), (1, 1)]
 
-MX_STEP = 2
-
 FLOPS = 2 * B * T * C * H + 2 * 2 * B * len(BLOCKS) * K_PASS * K_PASS * H
 
 
@@ -89,22 +87,15 @@ def tile_retentionhead_pa_kernel(tc, q, k, x, Wv, out):
             )
             masked.append(masked_j)
 
-        def transpose_q_or_k(tiles_of_128_rows, name):
-            rows_ps = psum.tile([P, T], BF16, tag="transposed", bufs=2)
-            for r in range(T // P):
-                nc.tensor.transpose(rows_ps[:, r * P : (r + 1) * P], tiles_of_128_rows[:, r, :], ident_bf16[:])
-            rows_T = work.tile([P, T], BF16, tag=name, name=name)
-            nc.scalar.copy(out=rows_T[:], in_=rows_ps[:])
-            return rows_T
-
-        def transpose_q(b):
-            return transpose_q_or_k(q_sb[b][:], "qT")
-
-        def transpose_k(b):
-            return transpose_q_or_k(k_sb[b][:].rearrange("p g t h -> p (g t) h"), "kT")
-
-        qT = transpose_q(0)
-        kT = transpose_k(0)
+        def transpose_q_and_k(b, half):
+            qkT_ps = psum.tile([P, 2, K_PASS], BF16, tag="transposed", bufs=2)
+            for r in range(TILES):
+                nc.tensor.transpose(qkT_ps[:, 0, r * P : (r + 1) * P], q_sb[b][:, half * TILES + r, :], ident_bf16[:])
+            for t in range(PACK):
+                nc.tensor.transpose(qkT_ps[:, 1, t * P : (t + 1) * P], k_sb[b][:, half, t, :], ident_bf16[:])
+            qkT = work.tile([P, 2, K_PASS], BF16, tag="qkT", bufs=2 * GROUPS)
+            nc.scalar.copy(out=qkT[:], in_=qkT_ps[:])
+            return qkT
 
         wv_grouped = const.tile([P, C_PASSES, H, PACK], BF16, align_bytes=64)
         wv_codes = const.tile([P, C_PASSES * H], U32, align_bytes=64)
@@ -176,6 +167,8 @@ def tile_retentionhead_pa_kernel(tc, q, k, x, Wv, out):
             out_rows = out[b, block * K_PASS : (block + 1) * K_PASS, :]
             nc.sync.dma_start(out=out_rows.rearrange("(j p) h -> p j h", p=P), in_=o_sb[:])
 
+        qkT = [transpose_q_and_k(0, half) for half in range(GROUPS)]
+        next_qkT = []
         v_mx, w_mx = {}, {}
         old_v_mx, old_w_mx = {}, {}
         x_mx = None
@@ -183,51 +176,51 @@ def tile_retentionhead_pa_kernel(tc, q, k, x, Wv, out):
             for phase, (block, g) in enumerate(BLOCKS):
                 gap = (block - g) * K_PASS
                 with_x = phase < GROUPS
-                v_grouped = None
-                w_grouped = work.tile([P, K_PASS, PACK], BF16, tag="w_grouped", bufs=2, align_bytes=64)
+                w_grouped = work.tile([P, K_PASS, PACK], BF16, tag="w_grouped", align_bytes=64)
                 if with_x:
                     x_grouped = work.tile([P, PACK * C], BF16, tag="x_grouped", align_bytes=64)
+                for pair in range(TILES // 2):
+                    scores = {}
+                    for j in (2 * pair, 2 * pair + 1):
+                        s_ps = psum.tile([P, PACK, P], F32, tag="s_ps", bufs=4)
+                        for t in range(PACK):
+                            nc.tensor.matmul(
+                                out=s_ps[:, t, :],
+                                lhsT=qkT[g][:, 1, t * P : (t + 1) * P],
+                                rhs=qkT[block][:, 0, j * P : (j + 1) * P],
+                                start=True,
+                                stop=True,
+                            )
+                        scores[j] = s_ps
+                    if with_x:
+                        for j in (2 * pair, 2 * pair + 1):
+                            transpose_x(b, phase, j, x_grouped)
+                    elif b + 1 < B:
+                        next_qkT.append(transpose_q_and_k(b + 1, pair))
+                    for j in (2 * pair, 2 * pair + 1):
+                        nc.vector.scalar_tensor_tensor(
+                            out=w_grouped[:, j * P : (j + 1) * P, :],
+                            in0=scores[j][:].rearrange("p t c -> p c t"),
+                            scalar=SCALE * GAMMA ** (gap + j * P),
+                            in1=(masked[j] if gap == 0 else decay)[:],
+                            op0=mybir.AluOpType.mult,
+                            op1=mybir.AluOpType.mult,
+                        )
+
+                v_grouped = None
+                if phase == 0 and b > 0:
+                    retain(b - 1, 1, old_w_mx, old_v_mx)
+                if phase == 1:
+                    v_grouped = project(x_mx[0], x_mx[1])
+                if phase == 2:
+                    retain(b, 0, w_mx, v_mx)
+                    v_grouped = project(x_mx[0], x_mx[1])
+
+                if with_x:
                     x_codes = work.tile([P, C], U32, tag="x_codes", align_bytes=64)
                     x_scales = work.tile([P, C], U8, tag="x_scales", align_bytes=64)
-                for j in range(TILES):
-                    queries = slice(block * K_PASS + j * P, block * K_PASS + (j + 1) * P)
-                    s_ps = psum.tile([P, PACK, P], F32, tag="s_ps", bufs=4)
-                    for t in range(PACK):
-                        col = (g * PACK + t) * P
-                        nc.tensor.matmul(
-                            out=s_ps[:, t, :], lhsT=kT[:, col : col + P], rhs=qT[:, queries], start=True, stop=True
-                        )
-                    if with_x:
-                        transpose_x(b, phase, j, x_grouped)
-                    if phase == GROUPS and b + 1 < B and j == 0:
-                        next_qT = transpose_q(b + 1)
-                    if phase == GROUPS and b + 1 < B and j == 1:
-                        next_kT = transpose_k(b + 1)
-                    if j == MX_STEP:
-                        if phase == 0 and b > 0:
-                            retain(b - 1, 1, old_w_mx, old_v_mx)
-                        if phase == 1:
-                            v_grouped = project(x_mx[0], x_mx[1])
-                        if phase == 2:
-                            retain(b, 0, w_mx, v_mx)
-                            v_grouped = project(x_mx[0], x_mx[1])
-                    nc.vector.scalar_tensor_tensor(
-                        out=w_grouped[:, j * P : (j + 1) * P, :],
-                        in0=s_ps[:].rearrange("p t c -> p c t"),
-                        scalar=SCALE * GAMMA ** (gap + j * P),
-                        in1=(masked[j] if gap == 0 else decay)[:],
-                        op0=mybir.AluOpType.mult,
-                        op1=mybir.AluOpType.mult,
-                    )
-                    if with_x:
-                        cols = slice(j * C_PASSES * P, (j + 1) * C_PASSES * P)
-                        nc.vector.quantize_mx(
-                            out=x_codes[:, cols].bitcast(FP8X4),
-                            scales=x_scales[:, cols],
-                            in_=x_grouped[:, j * C : (j + 1) * C],
-                        )
-                if b == 0 and phase == 0:
-                    quantise_wv()
+                    nc.vector.quantize_mx(out=x_codes[:].bitcast(FP8X4), scales=x_scales[:], in_=x_grouped[:])
+                    x_mx = (x_codes, x_scales)
                 w_codes = work.tile([P, K_PASS], U32, tag="w_codes", bufs=6, align_bytes=64)
                 w_scales = work.tile([P, K_PASS], U8, tag="w_scales", bufs=6, align_bytes=64)
                 nc.vector.quantize_mx(
@@ -245,10 +238,9 @@ def tile_retentionhead_pa_kernel(tc, q, k, x, Wv, out):
                         in_=v_grouped[:].rearrange("p h t -> p (h t)"),
                     )
                     v_mx[phase - 1] = (v_codes, v_scales)
-                if with_x:
-                    x_mx = (x_codes, x_scales)
+                if b == 0 and phase == 0:
+                    quantise_wv()
             old_v_mx, old_w_mx = v_mx, w_mx
             v_mx, w_mx = {}, {}
-            if b + 1 < B:
-                qT, kT = next_qT, next_kT
+            qkT, next_qkT = next_qkT, []
         retain(B - 1, 1, old_w_mx, old_v_mx)

@@ -22,6 +22,8 @@ TILES = K_PASS // P
 
 BLOCKS = [(0, 0), (1, 0), (1, 1)]
 
+SHARED_TILE = 0
+
 FLOPS = 2 * B * T * C * H + 2 * 2 * B * len(BLOCKS) * K_PASS * K_PASS * H
 
 
@@ -176,7 +178,7 @@ def tile_retentionhead_pa_kernel(tc, q, k, x, Wv, out):
             for phase, (block, g) in enumerate(BLOCKS):
                 gap = (block - g) * K_PASS
                 with_x = phase < GROUPS
-                w_grouped = work.tile([P, K_PASS, PACK], BF16, tag="w_grouped", align_bytes=64)
+                w_grouped = work.tile([P, K_PASS, PACK], BF16, tag="w_grouped", bufs=1, align_bytes=64)
                 if with_x:
                     x_grouped = work.tile([P, PACK * C], BF16, tag="x_grouped", align_bytes=64)
                 for pair in range(TILES // 2):
@@ -192,20 +194,32 @@ def tile_retentionhead_pa_kernel(tc, q, k, x, Wv, out):
                                 stop=True,
                             )
                         scores[j] = s_ps
+                        if j == SHARED_TILE:
+                            s_sb = work.tile([P, P, PACK], F32, tag="s_sb")
+                            nc.scalar.mul(
+                                out=s_sb[:], in_=s_ps[:].rearrange("p t c -> p c t"), mul=SCALE * GAMMA ** (gap + j * P)
+                            )
+                            nc.gpsimd.tensor_tensor(
+                                out=w_grouped[:, j * P : (j + 1) * P, :],
+                                in0=s_sb[:],
+                                in1=(masked[j] if gap == 0 else decay)[:],
+                                op=mybir.AluOpType.mult,
+                            )
                     if with_x:
                         for j in (2 * pair, 2 * pair + 1):
                             transpose_x(b, phase, j, x_grouped)
                     elif b + 1 < B:
                         next_qkT.append(transpose_q_and_k(b + 1, pair))
                     for j in (2 * pair, 2 * pair + 1):
-                        nc.vector.scalar_tensor_tensor(
-                            out=w_grouped[:, j * P : (j + 1) * P, :],
-                            in0=scores[j][:].rearrange("p t c -> p c t"),
-                            scalar=SCALE * GAMMA ** (gap + j * P),
-                            in1=(masked[j] if gap == 0 else decay)[:],
-                            op0=mybir.AluOpType.mult,
-                            op1=mybir.AluOpType.mult,
-                        )
+                        if j != SHARED_TILE:
+                            nc.vector.scalar_tensor_tensor(
+                                out=w_grouped[:, j * P : (j + 1) * P, :],
+                                in0=scores[j][:].rearrange("p t c -> p c t"),
+                                scalar=SCALE * GAMMA ** (gap + j * P),
+                                in1=(masked[j] if gap == 0 else decay)[:],
+                                op0=mybir.AluOpType.mult,
+                                op1=mybir.AluOpType.mult,
+                            )
 
                 v_grouped = None
                 if phase == 0 and b > 0:
@@ -221,14 +235,6 @@ def tile_retentionhead_pa_kernel(tc, q, k, x, Wv, out):
                     x_scales = work.tile([P, C], U8, tag="x_scales", align_bytes=64)
                     nc.vector.quantize_mx(out=x_codes[:].bitcast(FP8X4), scales=x_scales[:], in_=x_grouped[:])
                     x_mx = (x_codes, x_scales)
-                w_codes = work.tile([P, K_PASS], U32, tag="w_codes", bufs=6, align_bytes=64)
-                w_scales = work.tile([P, K_PASS], U8, tag="w_scales", bufs=6, align_bytes=64)
-                nc.vector.quantize_mx(
-                    out=w_codes[:].bitcast(FP8X4),
-                    scales=w_scales[:],
-                    in_=w_grouped[:].rearrange("p c t -> p (c t)"),
-                )
-                w_mx[(block, g)] = (w_codes, w_scales)
                 if v_grouped is not None:
                     v_codes = work.tile([P, H], U32, tag="v_codes", bufs=4, align_bytes=64)
                     v_scales = work.tile([P, H], U8, tag="v_scales", bufs=4, align_bytes=64)
@@ -240,6 +246,14 @@ def tile_retentionhead_pa_kernel(tc, q, k, x, Wv, out):
                     v_mx[phase - 1] = (v_codes, v_scales)
                 if b == 0 and phase == 0:
                     quantise_wv()
+                w_codes = work.tile([P, K_PASS], U32, tag="w_codes", bufs=6, align_bytes=64)
+                w_scales = work.tile([P, K_PASS], U8, tag="w_scales", bufs=6, align_bytes=64)
+                nc.vector.quantize_mx(
+                    out=w_codes[:].bitcast(FP8X4),
+                    scales=w_scales[:],
+                    in_=w_grouped[:].rearrange("p c t -> p (c t)"),
+                )
+                w_mx[(block, g)] = (w_codes, w_scales)
             old_v_mx, old_w_mx = v_mx, w_mx
             v_mx, w_mx = {}, {}
             qkT, next_qkT = next_qkT, []

@@ -38,26 +38,41 @@ def tile_retentionhead_pa_kernel(tc, q, k, x, Wv, out):
     ):
         wv_sb = loads.tile([P, C_PASSES * PACK, H], BF16)
         q_sb, k_sb, x_sb = [], [], []
-        for b in range(B):
-            q_tile = loads.tile([P, T // P, H], BF16, name="q%d" % b)
-            nc.sync.dma_start(out=q_tile[:], in_=q[b].rearrange("(r p) h -> p r h", p=P))
+
+        def load_q_and_k(b, half):
+            rows = slice(half * K_PASS, (half + 1) * K_PASS)
+            q_tile = loads.tile([P, TILES, H], BF16, name="q%d_%d" % (b, half))
+            nc.sync.dma_start(out=q_tile[:], in_=q[b, rows, :].rearrange("(r p) h -> p r h", p=P))
             q_sb.append(q_tile)
-            k_tile = loads.tile([P, GROUPS, PACK, H], BF16, name="k%d" % b)
+            k_tile = loads.tile([P, PACK, H], BF16, name="k%d_%d" % (b, half))
             nc.sync.dma_start(
-                out=k_tile[:].rearrange("p g t h -> p g (t h)"),
-                in_=k[b].rearrange("(g p t) h -> p g (t h)", p=P, t=PACK),
+                out=k_tile[:].rearrange("p t h -> p (t h)"),
+                in_=k[b, rows, :].rearrange("(p t) h -> p (t h)", t=PACK),
             )
             k_sb.append(k_tile)
-            for g in range(GROUPS):
-                x_tile = loads.tile([P, PACK * C], BF16, name="x%d_%d" % (b, g))
-                x_rows = x[b, g * K_PASS : (g + 1) * K_PASS, :]
-                nc.sync.dma_start(out=x_tile[:], in_=x_rows.rearrange("(p t) c -> p (t c)", t=PACK))
-                x_sb.append(x_tile)
-                if b == 0 and g == 0:
-                    nc.sync.dma_start(
-                        out=wv_sb[:].rearrange("w (a e) h -> w a (e h)", e=2),
-                        in_=Wv.rearrange("(a w e) h -> w a (e h)", w=P, e=2),
-                    )
+
+        def load_x(b, g, parts):
+            rows = x[b, g * K_PASS : (g + 1) * K_PASS, :].rearrange("(p t) c -> p t c", t=PACK)
+            tiles = []
+            for part in range(parts):
+                n = PACK // parts
+                x_tile = loads.tile([P, n, C], BF16, name="x%d_%d_%d" % (b, g, part))
+                nc.sync.dma_start(out=x_tile[:], in_=rows[:, part * n : (part + 1) * n, :])
+                tiles += [x_tile[:, i, :] for i in range(n)]
+            x_sb.append(tiles)
+
+        for b in range(B):
+            load_q_and_k(b, 0)
+            if b > 0:
+                load_q_and_k(b, 1)
+            load_x(b, 0, 4 if b == 0 else 1)
+            if b == 0:
+                load_q_and_k(b, 1)
+                nc.sync.dma_start(
+                    out=wv_sb[:].rearrange("w (a e) h -> w a (e h)", e=2),
+                    in_=Wv.rearrange("(a w e) h -> w a (e h)", w=P, e=2),
+                )
+            load_x(b, 1, 1)
 
         ident_bf16 = const.tile([P, P], BF16)
         make_identity(nc, ident_bf16[:])
@@ -90,11 +105,11 @@ def tile_retentionhead_pa_kernel(tc, q, k, x, Wv, out):
             masked.append(masked_j)
 
         def transpose_q_and_k(b, half):
-            qkT_ps = psum.tile([P, 2, K_PASS], BF16, tag="transposed", bufs=2)
+            qkT_ps = psum.tile([P, 2, K_PASS], BF16, tag="transposed", bufs=3)
             for r in range(TILES):
-                nc.tensor.transpose(qkT_ps[:, 0, r * P : (r + 1) * P], q_sb[b][:, half * TILES + r, :], ident_bf16[:])
+                nc.tensor.transpose(qkT_ps[:, 0, r * P : (r + 1) * P], q_sb[b * GROUPS + half][:, r, :], ident_bf16[:])
             for t in range(PACK):
-                nc.tensor.transpose(qkT_ps[:, 1, t * P : (t + 1) * P], k_sb[b][:, half, t, :], ident_bf16[:])
+                nc.tensor.transpose(qkT_ps[:, 1, t * P : (t + 1) * P], k_sb[b * GROUPS + half][:, t, :], ident_bf16[:])
             qkT = work.tile([P, 2, K_PASS], BF16, tag="qkT", bufs=2 * GROUPS)
             nc.scalar.copy(out=qkT[:], in_=qkT_ps[:])
             return qkT
@@ -118,11 +133,11 @@ def tile_retentionhead_pa_kernel(tc, q, k, x, Wv, out):
         words_per_row = C // 2
 
         def transpose_x(b, g, t, x_grouped):
-            x_words = x_sb[b * GROUPS + g][:].bitcast(F32)
-            xT = psum.tile([P, C_PASSES, 2, P], F32, tag="transposed", bufs=2)
+            x_words = x_sb[b * GROUPS + g][t].bitcast(F32)
+            xT = psum.tile([P, C_PASSES, 2, P], F32, tag="transposed", bufs=3)
             for G in range(C_PASSES):
                 for u in range(2):
-                    col = t * words_per_row + (G * 2 + u) * P
+                    col = (G * 2 + u) * P
                     nc.tensor.transpose(xT[:, G, u, :], x_words[:, col : col + P], ident_f32[:])
             nc.scalar.copy(
                 out=x_grouped[:]
@@ -169,72 +184,95 @@ def tile_retentionhead_pa_kernel(tc, q, k, x, Wv, out):
             out_rows = out[b, block * K_PASS : (block + 1) * K_PASS, :]
             nc.sync.dma_start(out=out_rows.rearrange("(j p) h -> p j h", p=P), in_=o_sb[:])
 
-        qkT = [transpose_q_and_k(0, half) for half in range(GROUPS)]
-        next_qkT = []
+        qkT = {0: transpose_q_and_k(0, 0)}
+        next_qkT = {}
         v_mx, w_mx = {}, {}
         old_v_mx, old_w_mx = {}, {}
-        x_mx = None
+        x_mx = {}
+        x_grouped = {}
+
+        def quantise_x(g, half):
+            cols = slice(half * PACK // 2 * C, (half + 1) * PACK // 2 * C)
+            words = slice(half * C // 2, (half + 1) * C // 2)
+            x_codes, x_scales = x_mx[g]
+            nc.vector.quantize_mx(
+                out=x_codes[:, words].bitcast(FP8X4), scales=x_scales[:, words], in_=x_grouped[g][:, cols]
+            )
+
+        def scores_of(j):
+            s_ps = psum.tile([P, PACK, P], F32, tag="s_ps", bufs=3)
+            for t in range(PACK):
+                nc.tensor.matmul(
+                    out=s_ps[:, t, :],
+                    lhsT=qkT[g][:, 1, t * P : (t + 1) * P],
+                    rhs=qkT[block][:, 0, j * P : (j + 1) * P],
+                    start=True,
+                    stop=True,
+                )
+            return s_ps
+
+        def multiply(j, s_ps):
+            nc.vector.scalar_tensor_tensor(
+                out=w_grouped[:, j * P : (j + 1) * P, :],
+                in0=s_ps[:].rearrange("p t c -> p c t"),
+                scalar=SCALE * GAMMA ** (gap + j * P),
+                in1=(masked[j] if gap == 0 else decay)[:],
+                op0=mybir.AluOpType.mult,
+                op1=mybir.AluOpType.mult,
+            )
+
         for b in range(B):
             for phase, (block, g) in enumerate(BLOCKS):
                 gap = (block - g) * K_PASS
                 with_x = phase < GROUPS
                 w_grouped = work.tile([P, K_PASS, PACK], BF16, tag="w_grouped", bufs=1, align_bytes=64)
                 if with_x:
-                    x_grouped = work.tile([P, PACK * C], BF16, tag="x_grouped", align_bytes=64)
-                for pair in range(TILES // 2):
-                    scores = {}
-                    for j in (2 * pair, 2 * pair + 1):
-                        s_ps = psum.tile([P, PACK, P], F32, tag="s_ps", bufs=4)
-                        for t in range(PACK):
-                            nc.tensor.matmul(
-                                out=s_ps[:, t, :],
-                                lhsT=qkT[g][:, 1, t * P : (t + 1) * P],
-                                rhs=qkT[block][:, 0, j * P : (j + 1) * P],
-                                start=True,
-                                stop=True,
-                            )
-                        scores[j] = s_ps
-                        if j == SHARED_TILE:
-                            s_sb = work.tile([P, P, PACK], F32, tag="s_sb")
-                            nc.scalar.mul(
-                                out=s_sb[:], in_=s_ps[:].rearrange("p t c -> p c t"), mul=SCALE * GAMMA ** (gap + j * P)
-                            )
-                            nc.gpsimd.tensor_tensor(
-                                out=w_grouped[:, j * P : (j + 1) * P, :],
-                                in0=s_sb[:],
-                                in1=(masked[j] if gap == 0 else decay)[:],
-                                op=mybir.AluOpType.mult,
-                            )
-                    if with_x:
-                        for j in (2 * pair, 2 * pair + 1):
-                            transpose_x(b, phase, j, x_grouped)
-                    elif b + 1 < B:
-                        next_qkT.append(transpose_q_and_k(b + 1, pair))
-                    for j in (2 * pair, 2 * pair + 1):
-                        if j != SHARED_TILE:
-                            nc.vector.scalar_tensor_tensor(
-                                out=w_grouped[:, j * P : (j + 1) * P, :],
-                                in0=scores[j][:].rearrange("p t c -> p c t"),
-                                scalar=SCALE * GAMMA ** (gap + j * P),
-                                in1=(masked[j] if gap == 0 else decay)[:],
-                                op0=mybir.AluOpType.mult,
-                                op1=mybir.AluOpType.mult,
-                            )
+                    x_tile_grouped = work.tile([P, PACK * C], BF16, tag="x_grouped", align_bytes=64)
+                    x_grouped[phase] = x_tile_grouped
+                    x_codes = work.tile([P, C], U32, tag="x_codes", align_bytes=64)
+                    x_scales = work.tile([P, C], U8, tag="x_scales", align_bytes=64)
+                    x_mx[phase] = (x_codes, x_scales)
+
+                s0 = scores_of(0)
+                s_sb = work.tile([P, P, PACK], F32, tag="s_sb")
+                nc.scalar.mul(out=s_sb[:], in_=s0[:].rearrange("p t c -> p c t"), mul=SCALE * GAMMA**gap)
+                nc.gpsimd.tensor_tensor(
+                    out=w_grouped[:, 0:P, :],
+                    in0=s_sb[:],
+                    in1=(masked[0] if gap == 0 else decay)[:],
+                    op=mybir.AluOpType.mult,
+                )
+                s1 = scores_of(1)
+                multiply(1, s1)
+                if with_x:
+                    transpose_x(b, phase, 0, x_grouped[phase])
+                    transpose_x(b, phase, 1, x_grouped[phase])
+                elif b + 1 < B:
+                    next_qkT[0] = transpose_q_and_k(b + 1, 0)
+                s2 = scores_of(2)
+                multiply(2, s2)
 
                 v_grouped = None
                 if phase == 0 and b > 0:
                     retain(b - 1, 1, old_w_mx, old_v_mx)
                 if phase == 1:
-                    v_grouped = project(x_mx[0], x_mx[1])
+                    v_grouped = project(*x_mx[0])
                 if phase == 2:
                     retain(b, 0, w_mx, v_mx)
-                    v_grouped = project(x_mx[0], x_mx[1])
+                    v_grouped = project(*x_mx[1])
+                s3 = scores_of(3)
+                multiply(3, s3)
+                if with_x:
+                    transpose_x(b, phase, 2, x_grouped[phase])
+                    transpose_x(b, phase, 3, x_grouped[phase])
+                elif b + 1 < B:
+                    next_qkT[1] = transpose_q_and_k(b + 1, 1)
+                if b == 0 and phase == 0:
+                    qkT[1] = transpose_q_and_k(0, 1)
+                    quantise_wv()
 
                 if with_x:
-                    x_codes = work.tile([P, C], U32, tag="x_codes", align_bytes=64)
-                    x_scales = work.tile([P, C], U8, tag="x_scales", align_bytes=64)
-                    nc.vector.quantize_mx(out=x_codes[:].bitcast(FP8X4), scales=x_scales[:], in_=x_grouped[:])
-                    x_mx = (x_codes, x_scales)
+                    quantise_x(phase, 0)
                 if v_grouped is not None:
                     v_codes = work.tile([P, H], U32, tag="v_codes", bufs=4, align_bytes=64)
                     v_scales = work.tile([P, H], U8, tag="v_scales", bufs=4, align_bytes=64)
@@ -244,8 +282,6 @@ def tile_retentionhead_pa_kernel(tc, q, k, x, Wv, out):
                         in_=v_grouped[:].rearrange("p h t -> p (h t)"),
                     )
                     v_mx[phase - 1] = (v_codes, v_scales)
-                if b == 0 and phase == 0:
-                    quantise_wv()
                 w_codes = work.tile([P, K_PASS], U32, tag="w_codes", bufs=6, align_bytes=64)
                 w_scales = work.tile([P, K_PASS], U8, tag="w_scales", bufs=6, align_bytes=64)
                 nc.vector.quantize_mx(
@@ -254,7 +290,9 @@ def tile_retentionhead_pa_kernel(tc, q, k, x, Wv, out):
                     in_=w_grouped[:].rearrange("p c t -> p (c t)"),
                 )
                 w_mx[(block, g)] = (w_codes, w_scales)
+                if with_x:
+                    quantise_x(phase, 1)
             old_v_mx, old_w_mx = v_mx, w_mx
             v_mx, w_mx = {}, {}
-            qkT, next_qkT = next_qkT, []
+            qkT, next_qkT = next_qkT, {}
         retain(B - 1, 1, old_w_mx, old_v_mx)

@@ -41,21 +41,23 @@ def tile_retentionhead_pa_kernel(tc, q, k, x, Wv, out):
 
         def load_q_and_k(b, half):
             rows = slice(half * K_PASS, (half + 1) * K_PASS)
-            q_tile = loads.tile([P, TILES, H], BF16, name="q%d_%d" % (b, half))
-            nc.sync.dma_start(out=q_tile[:], in_=q[b, rows, :].rearrange("(r p) h -> p r h", p=P))
-            q_sb.append(q_tile)
             k_tile = loads.tile([P, PACK, H], BF16, name="k%d_%d" % (b, half))
             nc.sync.dma_start(
                 out=k_tile[:].rearrange("p t h -> p (t h)"),
                 in_=k[b, rows, :].rearrange("(p t) h -> p (t h)", t=PACK),
             )
             k_sb.append(k_tile)
+            q_tile = loads.tile([P, TILES, H], BF16, name="q%d_%d" % (b, half))
+            nc.sync.dma_start(out=q_tile[:], in_=q[b, rows, :].rearrange("(r p) h -> p r h", p=P))
+            q_sb.append(q_tile)
 
         def load_x(b, g, parts):
             rows = x[b, g * K_PASS : (g + 1) * K_PASS, :].rearrange("(p t) c -> p t c", t=PACK)
             tiles = []
             for part in range(parts):
                 n = PACK // parts
+                if b == 0 and g == 0 and part == 2:
+                    load_q_and_k(b, 1)
                 x_tile = loads.tile([P, n, C], BF16, name="x%d_%d_%d" % (b, g, part))
                 nc.sync.dma_start(out=x_tile[:], in_=rows[:, part * n : (part + 1) * n, :])
                 tiles += [x_tile[:, i, :] for i in range(n)]
@@ -67,7 +69,6 @@ def tile_retentionhead_pa_kernel(tc, q, k, x, Wv, out):
                 load_q_and_k(b, 1)
             load_x(b, 0, 4 if b == 0 else 1)
             if b == 0:
-                load_q_and_k(b, 1)
                 nc.sync.dma_start(
                     out=wv_sb[:].rearrange("w (a e) h -> w a (e h)", e=2),
                     in_=Wv.rearrange("(a w e) h -> w a (e h)", w=P, e=2),
@@ -92,7 +93,12 @@ def tile_retentionhead_pa_kernel(tc, q, k, x, Wv, out):
             out=decay[:], in_=dist[:], func=mybir.ActivationFunctionType.Exp, scale=math.log(GAMMA)
         )
         masked = []
-        for j in range(TILES):
+
+        warm = psum.tile([P, TILES, P], F32, tag="s_ps", bufs=3)
+        for i in range(24):
+            nc.tensor.matmul(out=warm[:, i % TILES, :], lhsT=ident_bf16[:], rhs=ident_bf16[:], start=True, stop=True)
+
+        def mask_decay(j):
             masked_j = const.tile([P, P, PACK], F32, name="masked%d" % j)
             nc.vector.scalar_tensor_tensor(
                 out=masked_j[:],
@@ -106,12 +112,29 @@ def tile_retentionhead_pa_kernel(tc, q, k, x, Wv, out):
 
         def transpose_q_and_k(b, half):
             qkT_ps = psum.tile([P, 2, K_PASS], BF16, tag="transposed", bufs=3)
-            for r in range(TILES):
-                nc.tensor.transpose(qkT_ps[:, 0, r * P : (r + 1) * P], q_sb[b * GROUPS + half][:, r, :], ident_bf16[:])
             for t in range(PACK):
                 nc.tensor.transpose(qkT_ps[:, 1, t * P : (t + 1) * P], k_sb[b * GROUPS + half][:, t, :], ident_bf16[:])
+            for r in range(TILES):
+                nc.tensor.transpose(qkT_ps[:, 0, r * P : (r + 1) * P], q_sb[b * GROUPS + half][:, r, :], ident_bf16[:])
             qkT = work.tile([P, 2, K_PASS], BF16, tag="qkT", bufs=2 * GROUPS)
             nc.scalar.copy(out=qkT[:], in_=qkT_ps[:])
+            return qkT
+
+
+        def transpose_first_q_and_k():
+            qkT = work.tile([P, 2, K_PASS], BF16, tag="qkT", bufs=2 * GROUPS)
+            kT_ps = psum.tile([P, K_PASS], BF16, tag="transposed", bufs=3)
+            for t in range(PACK):
+                nc.tensor.transpose(kT_ps[:, t * P : (t + 1) * P], k_sb[0][:, t, :], ident_bf16[:])
+            nc.scalar.copy(out=qkT[:, 1, :], in_=kT_ps[:])
+            qT_ps = psum.tile([P, K_PASS], BF16, tag="transposed", bufs=3)
+            for r in range(TILES):
+                nc.tensor.transpose(qT_ps[:, r * P : (r + 1) * P], q_sb[0][:, r, :], ident_bf16[:])
+            mask_decay(0)
+            mask_decay(1)
+            nc.vector.tensor_copy(out=qkT[:, 0, :], in_=qT_ps[:])
+            mask_decay(2)
+            mask_decay(3)
             return qkT
 
         wv_grouped = const.tile([P, C_PASSES, H, PACK], BF16, align_bytes=64)
@@ -184,7 +207,7 @@ def tile_retentionhead_pa_kernel(tc, q, k, x, Wv, out):
             out_rows = out[b, block * K_PASS : (block + 1) * K_PASS, :]
             nc.sync.dma_start(out=out_rows.rearrange("(j p) h -> p j h", p=P), in_=o_sb[:])
 
-        qkT = {0: transpose_q_and_k(0, 0)}
+        qkT = {0: transpose_first_q_and_k()}
         next_qkT = {}
         v_mx, w_mx = {}, {}
         old_v_mx, old_w_mx = {}, {}
@@ -251,6 +274,8 @@ def tile_retentionhead_pa_kernel(tc, q, k, x, Wv, out):
                     next_qkT[0] = transpose_q_and_k(b + 1, 0)
                 s2 = scores_of(2)
                 multiply(2, s2)
+                if b == 0 and phase == 0:
+                    qkT[1] = transpose_q_and_k(0, 1)
 
                 v_grouped = None
                 if phase == 0 and b > 0:
@@ -268,7 +293,6 @@ def tile_retentionhead_pa_kernel(tc, q, k, x, Wv, out):
                 elif b + 1 < B:
                     next_qkT[1] = transpose_q_and_k(b + 1, 1)
                 if b == 0 and phase == 0:
-                    qkT[1] = transpose_q_and_k(0, 1)
                     quantise_wv()
 
                 if with_x:

@@ -202,7 +202,7 @@ def tile_retentionhead_pa_kernel(tc, q, k, x, Wv, out):
                         start=(g == 0),
                         stop=(g == block),
                     )
-            o_sb = work.tile([P, TILES, H], F32, tag="o_sb", bufs=3)
+            o_sb = work.tile([P, TILES, H], F32, tag="o_sb", bufs=8)
             nc.scalar.copy(out=o_sb[:], in_=o_ps[:])
             out_rows = out[b, block * K_PASS : (block + 1) * K_PASS, :]
             nc.sync.dma_start(out=out_rows.rearrange("(j p) h -> p j h", p=P), in_=o_sb[:])

@@ -48,7 +48,10 @@ def tile_retentionhead_pa_kernel(tc, q, k, x, Wv, out):
             )
             k_sb.append(k_tile)
             q_tile = loads.tile([P, TILES, H], BF16, name="q%d_%d" % (b, half))
-            nc.sync.dma_start(out=q_tile[:], in_=q[b, rows, :].rearrange("(r p) h -> p r h", p=P))
+            nc.sync.dma_start(
+                out=q_tile[:].rearrange("p j h -> p (j h)"),
+                in_=q[b, rows, :].rearrange("(p j) h -> p (j h)", j=TILES),
+            )
             q_sb.append(q_tile)
 
         def load_x(b, g, parts):
@@ -58,6 +61,11 @@ def tile_retentionhead_pa_kernel(tc, q, k, x, Wv, out):
                 n = PACK // parts
                 if b == 0 and g == 0 and part == 2:
                     load_q_and_k(b, 1)
+                if b == 0 and g == 1 and part == 1:
+                    nc.sync.dma_start(
+                        out=wv_sb[:].rearrange("w (a e) h -> w a (e h)", e=2),
+                        in_=Wv.rearrange("(a w e) h -> w a (e h)", w=P, e=2),
+                    )
                 x_tile = loads.tile([P, n, C], BF16, name="x%d_%d_%d" % (b, g, part))
                 nc.sync.dma_start(out=x_tile[:], in_=rows[:, part * n : (part + 1) * n, :])
                 tiles += [x_tile[:, i, :] for i in range(n)]
@@ -68,12 +76,7 @@ def tile_retentionhead_pa_kernel(tc, q, k, x, Wv, out):
             if b > 0:
                 load_q_and_k(b, 1)
             load_x(b, 0, 4 if b == 0 else 1)
-            if b == 0:
-                nc.sync.dma_start(
-                    out=wv_sb[:].rearrange("w (a e) h -> w a (e h)", e=2),
-                    in_=Wv.rearrange("(a w e) h -> w a (e h)", w=P, e=2),
-                )
-            load_x(b, 1, 1)
+            load_x(b, 1, 4 if b == 0 else 1)
 
         ident_bf16 = const.tile([P, P], BF16)
         make_identity(nc, ident_bf16[:])
@@ -83,7 +86,7 @@ def tile_retentionhead_pa_kernel(tc, q, k, x, Wv, out):
         dist = const.tile([P, P, PACK], F32)
         nc.gpsimd.iota(
             dist[:],
-            pattern=[[1, P], [-1, PACK]],
+            pattern=[[TILES, P], [-1, PACK]],
             base=0,
             channel_multiplier=-PACK,
             allow_small_or_imprecise_dtypes=True,
@@ -94,16 +97,12 @@ def tile_retentionhead_pa_kernel(tc, q, k, x, Wv, out):
         )
         masked = []
 
-        warm = psum.tile([P, TILES, P], F32, tag="s_ps", bufs=3)
-        for i in range(24):
-            nc.tensor.matmul(out=warm[:, i % TILES, :], lhsT=ident_bf16[:], rhs=ident_bf16[:], start=True, stop=True)
-
         def mask_decay(j):
             masked_j = const.tile([P, P, PACK], F32, name="masked%d" % j)
             nc.vector.scalar_tensor_tensor(
                 out=masked_j[:],
                 in0=dist[:],
-                scalar=float(-j * P),
+                scalar=float(-j),
                 in1=decay[:],
                 op0=mybir.AluOpType.is_ge,
                 op1=mybir.AluOpType.mult,
@@ -169,9 +168,8 @@ def tile_retentionhead_pa_kernel(tc, q, k, x, Wv, out):
                 in_=xT[:].rearrange("w G u p -> w G p u"),
             )
 
-        def project(x_codes, x_scales):
-            v_ps = psum.tile([P, PACK, H], F32, tag="v_ps")
-            for t in range(PACK):
+        def project(x_codes, x_scales, v_ps, slots):
+            for t in slots:
                 for G in range(C_PASSES):
                     cols = slice((t * C_PASSES + G) * P, (t * C_PASSES + G + 1) * P)
                     nc.tensor.matmul_mx(
@@ -183,6 +181,8 @@ def tile_retentionhead_pa_kernel(tc, q, k, x, Wv, out):
                         start=(G == 0),
                         stop=(G == C_PASSES - 1),
                     )
+
+        def round_v(v_ps):
             v_grouped = work.tile([P, H, PACK], BF16, tag="v_grouped", align_bytes=64)
             nc.scalar.copy(out=v_grouped[:], in_=v_ps[:].rearrange("p t h -> p h t"))
             return v_grouped
@@ -205,24 +205,36 @@ def tile_retentionhead_pa_kernel(tc, q, k, x, Wv, out):
             o_sb = work.tile([P, TILES, H], F32, tag="o_sb", bufs=8)
             nc.scalar.copy(out=o_sb[:], in_=o_ps[:])
             out_rows = out[b, block * K_PASS : (block + 1) * K_PASS, :]
-            nc.sync.dma_start(out=out_rows.rearrange("(j p) h -> p j h", p=P), in_=o_sb[:])
+            nc.sync.dma_start(out=out_rows.rearrange("(p j) h -> p j h", j=TILES), in_=o_sb[:])
+
+        def retain_half(b, half, w_mx, v_mx):
+            o_ps = psum.tile([P, TILES // 2, H], F32, tag="transposed", bufs=3)
+            for i in range(TILES // 2):
+                j = half * TILES // 2 + i
+                for g in range(GROUPS):
+                    w_codes, w_scales = w_mx[(1, g)]
+                    v_codes, v_scales = v_mx[g]
+                    nc.tensor.matmul_mx(
+                        out=o_ps[:, i, :],
+                        lhsT=w_codes[:, j * P : (j + 1) * P].bitcast(FP8X4),
+                        lhsT_scale=w_scales[:, j * P : (j + 1) * P],
+                        rhs=v_codes[:].bitcast(FP8X4),
+                        rhs_scale=v_scales[:],
+                        start=(g == 0),
+                        stop=(g == 1),
+                    )
+            o_half = work.tile([P, TILES // 2, H], F32, tag="o_half", bufs=2)
+            nc.scalar.copy(out=o_half[:], in_=o_ps[:])
+            out_rows = out[b, K_PASS : 2 * K_PASS, :].rearrange("(p j) h -> p j h", j=TILES)
+            nc.sync.dma_start(out=out_rows[:, half * TILES // 2 : (half + 1) * TILES // 2, :], in_=o_half[:])
 
         qkT = {0: transpose_first_q_and_k()}
         next_qkT = {}
-        v_mx, w_mx = {}, {}
+        v_mx, w_mx, x_mx, x_grouped = {}, {}, {}, {}
         old_v_mx, old_w_mx = {}, {}
-        x_mx = {}
-        x_grouped = {}
+        bank = {}
 
-        def quantise_x(g, half):
-            cols = slice(half * PACK // 2 * C, (half + 1) * PACK // 2 * C)
-            words = slice(half * C // 2, (half + 1) * C // 2)
-            x_codes, x_scales = x_mx[g]
-            nc.vector.quantize_mx(
-                out=x_codes[:, words].bitcast(FP8X4), scales=x_scales[:, words], in_=x_grouped[g][:, cols]
-            )
-
-        def scores_of(j):
+        def score(j):
             s_ps = psum.tile([P, PACK, P], F32, tag="s_ps", bufs=3)
             for t in range(PACK):
                 nc.tensor.matmul(
@@ -232,91 +244,118 @@ def tile_retentionhead_pa_kernel(tc, q, k, x, Wv, out):
                     start=True,
                     stop=True,
                 )
-            return s_ps
+            table = masked[j] if gap == 0 else decay
+            factor = SCALE * GAMMA ** (gap + j)
+            if j == SHARED_TILE:
+                s_sb = work.tile([P, P, PACK], F32, tag="s_sb")
+                nc.scalar.mul(out=s_sb[:], in_=s_ps[:].rearrange("p t c -> p c t"), mul=factor)
+                nc.gpsimd.tensor_tensor(
+                    out=w_grouped[:, j * P : (j + 1) * P, :], in0=s_sb[:], in1=table[:], op=mybir.AluOpType.mult
+                )
+            else:
+                nc.vector.scalar_tensor_tensor(
+                    out=w_grouped[:, j * P : (j + 1) * P, :],
+                    in0=s_ps[:].rearrange("p t c -> p c t"),
+                    scalar=factor,
+                    in1=table[:],
+                    op0=mybir.AluOpType.mult,
+                    op1=mybir.AluOpType.mult,
+                )
 
-        def multiply(j, s_ps):
-            nc.vector.scalar_tensor_tensor(
-                out=w_grouped[:, j * P : (j + 1) * P, :],
-                in0=s_ps[:].rearrange("p t c -> p c t"),
-                scalar=SCALE * GAMMA ** (gap + j * P),
-                in1=(masked[j] if gap == 0 else decay)[:],
-                op0=mybir.AluOpType.mult,
-                op1=mybir.AluOpType.mult,
+        def next_q_and_k(half):
+            if b + 1 < B:
+                next_qkT[half] = transpose_q_and_k(b + 1, half)
+
+        def first_q_and_k_half_1():
+            qkT[1] = transpose_q_and_k(0, 1)
+
+        def out_1_of_last_batch():
+            if b > 0:
+                retain(b - 1, 1, old_w_mx, old_v_mx)
+
+        def project_slots(slots):
+            if slots[0] == 0:
+                v_ps = psum.tile([P, PACK, H], F32, tag="v_ps")
+                bank["v"] = v_ps
+            project(*x_mx[phase - 1], bank["v"], slots)
+            if slots[-1] == PACK - 1:
+                bank["v_grouped"] = round_v(bank["v"])
+
+        def quantise_x(half):
+            cols = slice(half * PACK // 2 * C, (half + 1) * PACK // 2 * C)
+            words = slice(half * C // 2, (half + 1) * C // 2)
+            x_codes, x_scales = x_mx[phase]
+            nc.vector.quantize_mx(
+                out=x_codes[:, words].bitcast(FP8X4), scales=x_scales[:, words], in_=x_grouped[phase][:, cols]
             )
 
+        def quantise_v():
+            v_codes = work.tile([P, H], U32, tag="v_codes", bufs=4, align_bytes=64)
+            v_scales = work.tile([P, H], U8, tag="v_scales", bufs=4, align_bytes=64)
+            nc.vector.quantize_mx(
+                out=v_codes[:].bitcast(FP8X4),
+                scales=v_scales[:],
+                in_=bank["v_grouped"][:].rearrange("p h t -> p (h t)"),
+            )
+            v_mx[phase - 1] = (v_codes, v_scales)
+
+        def quantise_w(part, parts):
+            cols = slice(part * K_PASS // parts, (part + 1) * K_PASS // parts)
+            nc.vector.quantize_mx(
+                out=w_codes[:, cols].bitcast(FP8X4),
+                scales=w_scales[:, cols],
+                in_=w_grouped[:, cols, :].rearrange("p c t -> p (c t)"),
+            )
+
+        STEPS = {
+            "s0": lambda: score(0),
+            "s1": lambda: score(1),
+            "s2": lambda: score(2),
+            "s3": lambda: score(3),
+            "x0": lambda: transpose_x(b, phase, 0, x_grouped[phase]),
+            "x1": lambda: transpose_x(b, phase, 1, x_grouped[phase]),
+            "x2": lambda: transpose_x(b, phase, 2, x_grouped[phase]),
+            "x3": lambda: transpose_x(b, phase, 3, x_grouped[phase]),
+            "q0": lambda: next_q_and_k(0),
+            "q1": lambda: next_q_and_k(1),
+            "h1": first_q_and_k_half_1,
+            "R0": lambda: retain(b, 0, w_mx, v_mx),
+            "R1": out_1_of_last_batch,
+            "p01": lambda: project_slots((0, 1)),
+            "p23": lambda: project_slots((2, 3)),
+            "p0123": lambda: project_slots((0, 1, 2, 3)),
+            "X0": lambda: quantise_x(0),
+            "X1": lambda: quantise_x(1),
+            "VQ": quantise_v,
+            "WQ": lambda: quantise_w(0, 1),
+            "WH0": lambda: quantise_w(0, 2),
+            "WH1": lambda: quantise_w(1, 2),
+            "T0": lambda: retain_half(b, 0, w_mx, v_mx),
+            "T1": lambda: retain_half(b, 1, w_mx, v_mx),
+            "WV": quantise_wv,
+        }
+        PLANS = {
+            0: "s0 s1 x0 x1 s2 R1 s3 x2 x3 X0 WQ X1",
+            1: "s0 s1 x0 x1 s2 p01 s3 p23 x2 x3 X0 VQ WQ X1",
+            2: "s0 s1 q0 s2 R0 p01 s3 p23 q1 VQ WQ",
+            (3, 2): "s0 s1 s2 R0 p01 s3 p23 VQ WH0 T0 WH1 T1",
+            (0, 0): "x0 s0 s1 x1 s2 h1 s3 x2 x3 X0 WV WQ X1",
+        }
         for b in range(B):
             for phase, (block, g) in enumerate(BLOCKS):
                 gap = (block - g) * K_PASS
-                with_x = phase < GROUPS
                 w_grouped = work.tile([P, K_PASS, PACK], BF16, tag="w_grouped", bufs=1, align_bytes=64)
-                if with_x:
-                    x_tile_grouped = work.tile([P, PACK * C], BF16, tag="x_grouped", align_bytes=64)
-                    x_grouped[phase] = x_tile_grouped
-                    x_codes = work.tile([P, C], U32, tag="x_codes", align_bytes=64)
-                    x_scales = work.tile([P, C], U8, tag="x_scales", align_bytes=64)
-                    x_mx[phase] = (x_codes, x_scales)
-
-                s0 = scores_of(0)
-                s_sb = work.tile([P, P, PACK], F32, tag="s_sb")
-                nc.scalar.mul(out=s_sb[:], in_=s0[:].rearrange("p t c -> p c t"), mul=SCALE * GAMMA**gap)
-                nc.gpsimd.tensor_tensor(
-                    out=w_grouped[:, 0:P, :],
-                    in0=s_sb[:],
-                    in1=(masked[0] if gap == 0 else decay)[:],
-                    op=mybir.AluOpType.mult,
-                )
-                s1 = scores_of(1)
-                multiply(1, s1)
-                if with_x:
-                    transpose_x(b, phase, 0, x_grouped[phase])
-                    transpose_x(b, phase, 1, x_grouped[phase])
-                elif b + 1 < B:
-                    next_qkT[0] = transpose_q_and_k(b + 1, 0)
-                s2 = scores_of(2)
-                multiply(2, s2)
-                if b == 0 and phase == 0:
-                    qkT[1] = transpose_q_and_k(0, 1)
-
-                v_grouped = None
-                if phase == 0 and b > 0:
-                    retain(b - 1, 1, old_w_mx, old_v_mx)
-                if phase == 1:
-                    v_grouped = project(*x_mx[0])
-                if phase == 2:
-                    retain(b, 0, w_mx, v_mx)
-                    v_grouped = project(*x_mx[1])
-                s3 = scores_of(3)
-                multiply(3, s3)
-                if with_x:
-                    transpose_x(b, phase, 2, x_grouped[phase])
-                    transpose_x(b, phase, 3, x_grouped[phase])
-                elif b + 1 < B:
-                    next_qkT[1] = transpose_q_and_k(b + 1, 1)
-                if b == 0 and phase == 0:
-                    quantise_wv()
-
-                if with_x:
-                    quantise_x(phase, 0)
-                if v_grouped is not None:
-                    v_codes = work.tile([P, H], U32, tag="v_codes", bufs=4, align_bytes=64)
-                    v_scales = work.tile([P, H], U8, tag="v_scales", bufs=4, align_bytes=64)
-                    nc.vector.quantize_mx(
-                        out=v_codes[:].bitcast(FP8X4),
-                        scales=v_scales[:],
-                        in_=v_grouped[:].rearrange("p h t -> p (h t)"),
-                    )
-                    v_mx[phase - 1] = (v_codes, v_scales)
                 w_codes = work.tile([P, K_PASS], U32, tag="w_codes", bufs=6, align_bytes=64)
                 w_scales = work.tile([P, K_PASS], U8, tag="w_scales", bufs=6, align_bytes=64)
-                nc.vector.quantize_mx(
-                    out=w_codes[:].bitcast(FP8X4),
-                    scales=w_scales[:],
-                    in_=w_grouped[:].rearrange("p c t -> p (c t)"),
-                )
                 w_mx[(block, g)] = (w_codes, w_scales)
-                if with_x:
-                    quantise_x(phase, 1)
+                if phase < GROUPS:
+                    x_words_grouped = work.tile([P, PACK * C], BF16, tag="x_grouped", align_bytes=64)
+                    x_codes = work.tile([P, C], U32, tag="x_codes", align_bytes=64)
+                    x_scales = work.tile([P, C], U8, tag="x_scales", align_bytes=64)
+                    x_grouped[phase] = x_words_grouped
+                    x_mx[phase] = (x_codes, x_scales)
+                for step in PLANS.get((b, phase), PLANS[phase]).split():
+                    STEPS[step]()
             old_v_mx, old_w_mx = v_mx, w_mx
             v_mx, w_mx = {}, {}
             qkT, next_qkT = next_qkT, {}
-        retain(B - 1, 1, old_w_mx, old_v_mx)

@@ -335,9 +335,9 @@ def tile_retentionhead_pa_kernel(tc, q, k, x, Wv, out):
             "WV": quantise_wv,
         }
         PLANS = {
-            0: "s0 s1 x0 x1 s2 R1 s3 x2 x3 X0 WQ X1",
-            1: "s0 s1 x0 x1 s2 p01 s3 p23 x2 x3 X0 VQ WQ X1",
-            2: "s0 s1 q0 s2 R0 p01 s3 p23 q1 VQ WQ",
+            0: "s0 s1 x0 x1 x2 s2 R1 s3 x3 X0 WQ X1",
+            1: "s0 s1 x0 x1 x2 s2 p01 s3 p23 x3 X0 VQ WQ X1",
+            2: "s0 s1 q0 q1 s2 R0 p01 s3 p23 VQ WQ",
             (3, 2): "s0 s1 s2 R0 p01 s3 p23 VQ WH0 T0 WH1 T1",
             (0, 0): "x0 s0 s1 x1 s2 h1 s3 x2 x3 X0 WV WQ X1",
         }

@@ -129,11 +129,9 @@ def tile_retentionhead_pa_kernel(tc, q, k, x, Wv, out):
             qT_ps = psum.tile([P, K_PASS], BF16, tag="transposed", bufs=3)
             for r in range(TILES):
                 nc.tensor.transpose(qT_ps[:, r * P : (r + 1) * P], q_sb[0][:, r, :], ident_bf16[:])
-            mask_decay(0)
-            mask_decay(1)
-            nc.vector.tensor_copy(out=qkT[:, 0, :], in_=qT_ps[:])
-            mask_decay(2)
-            mask_decay(3)
+            nc.scalar.copy(out=qkT[:, 0, :], in_=qT_ps[:])
+            for j in range(TILES):
+                mask_decay(j)
             return qkT
 
         wv_grouped = const.tile([P, C_PASSES, H, PACK], BF16, align_bytes=64)
@@ -336,8 +334,8 @@ def tile_retentionhead_pa_kernel(tc, q, k, x, Wv, out):
         }
         PLANS = {
             0: "s0 s1 x0 x1 x2 s2 R1 s3 x3 X0 WQ X1",
-            1: "s0 s1 x0 x1 x2 s2 p01 s3 p23 x3 X0 VQ WQ X1",
-            2: "s0 s1 q0 q1 s2 R0 p01 s3 p23 VQ WQ",
+            1: "s0 s1 x0 x1 x2 s2 s3 p01 p23 x3 X0 VQ WQ X1",
+            2: "s0 s1 q0 q1 s2 s3 R0 p01 p23 VQ WQ",
             (3, 2): "s0 s1 s2 R0 p01 s3 p23 VQ WH0 T0 WH1 T1",
             (0, 0): "x0 s0 s1 x1 s2 h1 s3 x2 x3 X0 WV WQ X1",
         }

@@ -110,7 +110,7 @@ def tile_retentionhead_pa_kernel(tc, q, k, x, Wv, out):
             masked.append(masked_j)
 
         def transpose_q_and_k(b, half):
-            qkT_ps = psum.tile([P, 2, K_PASS], BF16, tag="transposed", bufs=3)
+            qkT_ps = psum.tile([P, 2, K_PASS], BF16, tag="sbank", bufs=5)
             for t in range(PACK):
                 nc.tensor.transpose(qkT_ps[:, 1, t * P : (t + 1) * P], k_sb[b * GROUPS + half][:, t, :], ident_bf16[:])
             for r in range(TILES):
@@ -122,11 +122,11 @@ def tile_retentionhead_pa_kernel(tc, q, k, x, Wv, out):
 
         def transpose_first_q_and_k():
             qkT = work.tile([P, 2, K_PASS], BF16, tag="qkT", bufs=2 * GROUPS)
-            kT_ps = psum.tile([P, K_PASS], BF16, tag="transposed", bufs=3)
+            kT_ps = psum.tile([P, K_PASS], BF16, tag="sbank", bufs=5)
             for t in range(PACK):
                 nc.tensor.transpose(kT_ps[:, t * P : (t + 1) * P], k_sb[0][:, t, :], ident_bf16[:])
             nc.scalar.copy(out=qkT[:, 1, :], in_=kT_ps[:])
-            qT_ps = psum.tile([P, K_PASS], BF16, tag="transposed", bufs=3)
+            qT_ps = psum.tile([P, K_PASS], BF16, tag="sbank", bufs=5)
             for r in range(TILES):
                 nc.tensor.transpose(qT_ps[:, r * P : (r + 1) * P], q_sb[0][:, r, :], ident_bf16[:])
             nc.scalar.copy(out=qkT[:, 0, :], in_=qT_ps[:])
@@ -154,7 +154,7 @@ def tile_retentionhead_pa_kernel(tc, q, k, x, Wv, out):
 
         def transpose_x(b, g, t, x_grouped):
             x_words = x_sb[b * GROUPS + g][t].bitcast(F32)
-            xT = psum.tile([P, C_PASSES, 2, P], F32, tag="transposed", bufs=3)
+            xT = psum.tile([P, C_PASSES, 2, P], F32, tag="sbank", bufs=5)
             for G in range(C_PASSES):
                 for u in range(2):
                     col = (G * 2 + u) * P
@@ -186,7 +186,7 @@ def tile_retentionhead_pa_kernel(tc, q, k, x, Wv, out):
             return v_grouped
 
         def retain(b, block, w_mx, v_mx):
-            o_ps = psum.tile([P, TILES, H], F32, tag="o_ps")
+            o_ps = psum.tile([P, TILES, H], F32, tag="sbank", bufs=5)
             for j in range(TILES):
                 for g in range(block + 1):
                     w_codes, w_scales = w_mx[(block, g)]
@@ -206,7 +206,7 @@ def tile_retentionhead_pa_kernel(tc, q, k, x, Wv, out):
             nc.sync.dma_start(out=out_rows.rearrange("(p j) h -> p j h", j=TILES), in_=o_sb[:])
 
         def retain_half(b, half, w_mx, v_mx):
-            o_ps = psum.tile([P, TILES // 2, H], F32, tag="transposed", bufs=3)
+            o_ps = psum.tile([P, TILES // 2, H], F32, tag="sbank", bufs=5)
             for i in range(TILES // 2):
                 j = half * TILES // 2 + i
                 for g in range(GROUPS):
@@ -233,7 +233,8 @@ def tile_retentionhead_pa_kernel(tc, q, k, x, Wv, out):
         bank = {}
 
         def score(j):
-            s_ps = psum.tile([P, PACK, P], F32, tag="s_ps", bufs=3)
+            shared = j == SHARED_TILE
+            s_ps = psum.tile([P, PACK, P], F32, tag=("sbank" if shared else "s_ps"), bufs=(5 if shared else 3), name="s_ps")
             for t in range(PACK):
                 nc.tensor.matmul(
                     out=s_ps[:, t, :],
@@ -273,7 +274,7 @@ def tile_retentionhead_pa_kernel(tc, q, k, x, Wv, out):
 
         def project_slots(slots):
             if slots[0] == 0:
-                v_ps = psum.tile([P, PACK, H], F32, tag="v_ps")
+                v_ps = psum.tile([P, PACK, H], F32, tag="sbank", bufs=5)
                 bank["v"] = v_ps
             project(*x_mx[phase - 1], bank["v"], slots)
             if slots[-1] == PACK - 1:
@@ -333,10 +334,10 @@ def tile_retentionhead_pa_kernel(tc, q, k, x, Wv, out):
             "WV": quantise_wv,
         }
         PLANS = {
-            0: "s0 s1 x0 x1 x2 s2 R1 s3 x3 X0 WQ X1",
-            1: "s0 s1 x0 x1 x2 s2 s3 p01 p23 x3 X0 VQ WQ X1",
+            0: "s0 s1 x0 x1 x2 x3 s2 s3 R1 X0 WQ X1",
+            1: "s0 s1 x0 x1 x2 x3 s2 s3 p01 p23 X0 VQ WQ X1",
             2: "s0 s1 q0 q1 s2 s3 R0 p01 p23 VQ WQ",
-            (3, 2): "s0 s1 s2 R0 p01 s3 p23 VQ WH0 T0 WH1 T1",
+            (3, 2): "s0 s1 s2 s3 p01 p23 R0 VQ WH0 T0 WH1 T1",
             (0, 0): "x0 s0 s1 x1 s2 h1 s3 x2 x3 X0 WV WQ X1",
         }
         for b in range(B):

import math

import concourse.mybir as mybir
from concourse.masks import make_identity

F32 = mybir.dt.float32
BF16 = mybir.dt.bfloat16
U32 = mybir.dt.uint32
U8 = mybir.dt.uint8
FP8X4 = mybir.dt.float8_e4m3fn_x4

B, T, C, H = 4, 1024, 1024, 128
GAMMA = 0.96875
SCALE = C**-0.5

P = 128
PACK = 4
K_PASS = P * PACK
GROUPS = T // K_PASS
C_PASSES = C // K_PASS
TILES = K_PASS // P

BLOCKS = [(0, 0), (1, 0), (1, 1)]

SHARED_TILE = 0

FLOPS = 2 * B * T * C * H + 2 * 2 * B * len(BLOCKS) * K_PASS * K_PASS * H


def tile_retentionhead_pa_kernel(tc, q, k, x, Wv, out):
    nc = tc.nc
    with (
        tc.tile_pool(name="loads", bufs=1) as loads,
        tc.tile_pool(name="const", bufs=1) as const,
        tc.tile_pool(name="work", bufs=2) as work,
        tc.psum_pool(name="psum", bufs=1) as psum,
        tc.manual_schedule(),
    ):
        wv_sb = loads.tile([P, C_PASSES * PACK, H], BF16)
        q_sb, k_sb, x_sb = [], [], []

        def load_q_and_k(b, half):
            rows = slice(half * K_PASS, (half + 1) * K_PASS)
            k_tile = loads.tile([P, PACK, H], BF16, name="k%d_%d" % (b, half))
            nc.sync.dma_start(
                out=k_tile[:].rearrange("p t h -> p (t h)"),
                in_=k[b, rows, :].rearrange("(p t) h -> p (t h)", t=PACK),
            )
            k_sb.append(k_tile)
            q_tile = loads.tile([P, TILES, H], BF16, name="q%d_%d" % (b, half))
            nc.sync.dma_start(
                out=q_tile[:].rearrange("p j h -> p (j h)"),
                in_=q[b, rows, :].rearrange("(p j) h -> p (j h)", j=TILES),
            )
            q_sb.append(q_tile)

        def load_x(b, g, parts):
            rows = x[b, g * K_PASS : (g + 1) * K_PASS, :].rearrange("(p t) c -> p t c", t=PACK)
            tiles = []
            for part in range(parts):
                n = PACK // parts
                if b == 0 and g == 0 and part == 2:
                    load_q_and_k(b, 1)
                if b == 0 and g == 1 and part == 1:
                    nc.sync.dma_start(
                        out=wv_sb[:].rearrange("w (a e) h -> w a (e h)", e=2),
                        in_=Wv.rearrange("(a w e) h -> w a (e h)", w=P, e=2),
                    )
                x_tile = loads.tile([P, n, C], BF16, name="x%d_%d_%d" % (b, g, part))
                nc.sync.dma_start(out=x_tile[:], in_=rows[:, part * n : (part + 1) * n, :])
                tiles += [x_tile[:, i, :] for i in range(n)]
            x_sb.append(tiles)

        for b in range(B):
            load_q_and_k(b, 0)
            if b > 0:
                load_q_and_k(b, 1)
            load_x(b, 0, 4 if b == 0 else 1)
            load_x(b, 1, 4 if b == 0 else 1)

        ident_bf16 = const.tile([P, P], BF16)
        make_identity(nc, ident_bf16[:])
        ident_f32 = const.tile([P, P], F32)
        nc.vector.tensor_copy(out=ident_f32[:], in_=ident_bf16[:])

        dist = const.tile([P, P, PACK], F32)
        nc.gpsimd.iota(
            dist[:],
            pattern=[[TILES, P], [-1, PACK]],
            base=0,
            channel_multiplier=-PACK,
            allow_small_or_imprecise_dtypes=True,
        )
        decay = const.tile([P, P, PACK], F32)
        nc.scalar.activation(
            out=decay[:], in_=dist[:], func=mybir.ActivationFunctionType.Exp, scale=math.log(GAMMA)
        )
        masked = []

        def mask_decay(j):
            masked_j = const.tile([P, P, PACK], F32, name="masked%d" % j)
            nc.vector.scalar_tensor_tensor(
                out=masked_j[:],
                in0=dist[:],
                scalar=float(-j),
                in1=decay[:],
                op0=mybir.AluOpType.is_ge,
                op1=mybir.AluOpType.mult,
            )
            masked.append(masked_j)

        def transpose_q_and_k(b, half):
            qkT_ps = psum.tile([P, 2, K_PASS], BF16, tag="sbank", bufs=5)
            for t in range(PACK):
                nc.tensor.transpose(qkT_ps[:, 1, t * P : (t + 1) * P], k_sb[b * GROUPS + half][:, t, :], ident_bf16[:])
            for r in range(TILES):
                nc.tensor.transpose(qkT_ps[:, 0, r * P : (r + 1) * P], q_sb[b * GROUPS + half][:, r, :], ident_bf16[:])
            qkT = work.tile([P, 2, K_PASS], BF16, tag="qkT", bufs=2 * GROUPS)
            nc.scalar.copy(out=qkT[:], in_=qkT_ps[:])
            return qkT


        def transpose_first_q_and_k():
            qkT = work.tile([P, 2, K_PASS], BF16, tag="qkT", bufs=2 * GROUPS)
            kT_ps = psum.tile([P, K_PASS], BF16, tag="sbank", bufs=5)
            for t in range(PACK):
                nc.tensor.transpose(kT_ps[:, t * P : (t + 1) * P], k_sb[0][:, t, :], ident_bf16[:])
            nc.scalar.copy(out=qkT[:, 1, :], in_=kT_ps[:])
            qT_ps = psum.tile([P, K_PASS], BF16, tag="sbank", bufs=5)
            for r in range(TILES):
                nc.tensor.transpose(qT_ps[:, r * P : (r + 1) * P], q_sb[0][:, r, :], ident_bf16[:])
            nc.scalar.copy(out=qkT[:, 0, :], in_=qT_ps[:])
            for j in range(TILES):
                mask_decay(j)
            return qkT

        wv_grouped = const.tile([P, C_PASSES, H, PACK], BF16, align_bytes=64)
        wv_codes = const.tile([P, C_PASSES * H], U32, align_bytes=64)
        wv_scales = const.tile([P, C_PASSES * H], U8, align_bytes=64)

        def quantise_wv():
            for G in range(C_PASSES):
                nc.vector.tensor_copy(
                    out=wv_grouped[:, G],
                    in_=wv_sb[:, G * PACK : (G + 1) * PACK, :].rearrange("w s h -> w h s"),
                )
            nc.vector.quantize_mx(
                out=wv_codes[:].bitcast(FP8X4),
                scales=wv_scales[:],
                in_=wv_grouped[:].rearrange("w G h s -> w (G h s)"),
            )

        words_per_row = C // 2

        def transpose_x(b, g, t, x_grouped):
            x_words = x_sb[b * GROUPS + g][t].bitcast(F32)
            xT = psum.tile([P, C_PASSES, 2, P], F32, tag="sbank", bufs=5)
            for G in range(C_PASSES):
                for u in range(2):
                    col = (G * 2 + u) * P
                    nc.tensor.transpose(xT[:, G, u, :], x_words[:, col : col + P], ident_f32[:])
            nc.scalar.copy(
                out=x_grouped[:]
                .bitcast(F32)[:, t * words_per_row : (t + 1) * words_per_row]
                .rearrange("w (G p u) -> w G p u", G=C_PASSES, u=2),
                in_=xT[:].rearrange("w G u p -> w G p u"),
            )

        def project(x_codes, x_scales, v_ps, slots):
            for t in slots:
                for G in range(C_PASSES):
                    cols = slice((t * C_PASSES + G) * P, (t * C_PASSES + G + 1) * P)
                    nc.tensor.matmul_mx(
                        out=v_ps[:, t, :],
                        lhsT=x_codes[:, cols].bitcast(FP8X4),
                        lhsT_scale=x_scales[:, cols],
                        rhs=wv_codes[:, G * H : (G + 1) * H].bitcast(FP8X4),
                        rhs_scale=wv_scales[:, G * H : (G + 1) * H],
                        start=(G == 0),
                        stop=(G == C_PASSES - 1),
                    )

        def round_v(v_ps):
            v_grouped = work.tile([P, H, PACK], BF16, tag="v_grouped", align_bytes=64)
            nc.scalar.copy(out=v_grouped[:], in_=v_ps[:].rearrange("p t h -> p h t"))
            return v_grouped

        def retain(b, block, w_mx, v_mx):
            o_ps = psum.tile([P, TILES, H], F32, tag="sbank", bufs=5)
            for j in range(TILES):
                for g in range(block + 1):
                    w_codes, w_scales = w_mx[(block, g)]
                    v_codes, v_scales = v_mx[g]
                    nc.tensor.matmul_mx(
                        out=o_ps[:, j, :],
                        lhsT=w_codes[:, j * P : (j + 1) * P].bitcast(FP8X4),
                        lhsT_scale=w_scales[:, j * P : (j + 1) * P],
                        rhs=v_codes[:].bitcast(FP8X4),
                        rhs_scale=v_scales[:],
                        start=(g == 0),
                        stop=(g == block),
                    )
            o_sb = work.tile([P, TILES, H], F32, tag="o_sb", bufs=8)
            nc.scalar.copy(out=o_sb[:], in_=o_ps[:])
            out_rows = out[b, block * K_PASS : (block + 1) * K_PASS, :]
            nc.sync.dma_start(out=out_rows.rearrange("(p j) h -> p j h", j=TILES), in_=o_sb[:])

        def retain_half(b, half, w_mx, v_mx):
            o_ps = psum.tile([P, TILES // 2, H], F32, tag="sbank", bufs=5)
            for i in range(TILES // 2):
                j = half * TILES // 2 + i
                for g in range(GROUPS):
                    w_codes, w_scales = w_mx[(1, g)]
                    v_codes, v_scales = v_mx[g]
                    nc.tensor.matmul_mx(
                        out=o_ps[:, i, :],
                        lhsT=w_codes[:, j * P : (j + 1) * P].bitcast(FP8X4),
                        lhsT_scale=w_scales[:, j * P : (j + 1) * P],
                        rhs=v_codes[:].bitcast(FP8X4),
                        rhs_scale=v_scales[:],
                        start=(g == 0),
                        stop=(g == 1),
                    )
            o_half = work.tile([P, TILES // 2, H], F32, tag="o_half", bufs=2)
            nc.scalar.copy(out=o_half[:], in_=o_ps[:])
            out_rows = out[b, K_PASS : 2 * K_PASS, :].rearrange("(p j) h -> p j h", j=TILES)
            nc.sync.dma_start(out=out_rows[:, half * TILES // 2 : (half + 1) * TILES // 2, :], in_=o_half[:])

        qkT = {0: transpose_first_q_and_k()}
        next_qkT = {}
        v_mx, w_mx, x_mx, x_grouped = {}, {}, {}, {}
        old_v_mx, old_w_mx = {}, {}
        bank = {}

        def score(j):
            shared = j == SHARED_TILE
            s_ps = psum.tile([P, PACK, P], F32, tag=("sbank" if shared else "s_ps"), bufs=(5 if shared else 3), name="s_ps")
            for t in range(PACK):
                nc.tensor.matmul(
                    out=s_ps[:, t, :],
                    lhsT=qkT[g][:, 1, t * P : (t + 1) * P],
                    rhs=qkT[block][:, 0, j * P : (j + 1) * P],
                    start=True,
                    stop=True,
                )
            table = masked[j] if gap == 0 else decay
            factor = SCALE * GAMMA ** (gap + j)
            if j == SHARED_TILE:
                s_sb = work.tile([P, P, PACK], F32, tag="s_sb")
                nc.scalar.mul(out=s_sb[:], in_=s_ps[:].rearrange("p t c -> p c t"), mul=factor)
                nc.gpsimd.tensor_tensor(
                    out=w_grouped[:, j * P : (j + 1) * P, :], in0=s_sb[:], in1=table[:], op=mybir.AluOpType.mult
                )
            else:
                nc.vector.scalar_tensor_tensor(
                    out=w_grouped[:, j * P : (j + 1) * P, :],
                    in0=s_ps[:].rearrange("p t c -> p c t"),
                    scalar=factor,
                    in1=table[:],
                    op0=mybir.AluOpType.mult,
                    op1=mybir.AluOpType.mult,
                )

        def next_q_and_k(half):
            if b + 1 < B:
                next_qkT[half] = transpose_q_and_k(b + 1, half)

        def first_q_and_k_half_1():
            qkT[1] = transpose_q_and_k(0, 1)

        def out_1_of_last_batch():
            if b > 0:
                retain(b - 1, 1, old_w_mx, old_v_mx)

        def project_slots(slots):
            if slots[0] == 0:
                v_ps = psum.tile([P, PACK, H], F32, tag="sbank", bufs=5)
                bank["v"] = v_ps
            project(*x_mx[phase - 1], bank["v"], slots)
            if slots[-1] == PACK - 1:
                bank["v_grouped"] = round_v(bank["v"])

        def quantise_x(half):
            cols = slice(half * PACK // 2 * C, (half + 1) * PACK // 2 * C)
            words = slice(half * C // 2, (half + 1) * C // 2)
            x_codes, x_scales = x_mx[phase]
            nc.vector.quantize_mx(
                out=x_codes[:, words].bitcast(FP8X4), scales=x_scales[:, words], in_=x_grouped[phase][:, cols]
            )

        def quantise_v():
            v_codes = work.tile([P, H], U32, tag="v_codes", bufs=4, align_bytes=64)
            v_scales = work.tile([P, H], U8, tag="v_scales", bufs=4, align_bytes=64)
            nc.vector.quantize_mx(
                out=v_codes[:].bitcast(FP8X4),
                scales=v_scales[:],
                in_=bank["v_grouped"][:].rearrange("p h t -> p (h t)"),
            )
            v_mx[phase - 1] = (v_codes, v_scales)

        def quantise_w(part, parts):
            cols = slice(part * K_PASS // parts, (part + 1) * K_PASS // parts)
            nc.vector.quantize_mx(
                out=w_codes[:, cols].bitcast(FP8X4),
                scales=w_scales[:, cols],
                in_=w_grouped[:, cols, :].rearrange("p c t -> p (c t)"),
            )

        STEPS = {
            "s0": lambda: score(0),
            "s1": lambda: score(1),
            "s2": lambda: score(2),
            "s3": lambda: score(3),
            "x0": lambda: transpose_x(b, phase, 0, x_grouped[phase]),
            "x1": lambda: transpose_x(b, phase, 1, x_grouped[phase]),
            "x2": lambda: transpose_x(b, phase, 2, x_grouped[phase]),
            "x3": lambda: transpose_x(b, phase, 3, x_grouped[phase]),
            "q0": lambda: next_q_and_k(0),
            "q1": lambda: next_q_and_k(1),
            "h1": first_q_and_k_half_1,
            "R0": lambda: retain(b, 0, w_mx, v_mx),
            "R1": out_1_of_last_batch,
            "p01": lambda: project_slots((0, 1)),
            "p23": lambda: project_slots((2, 3)),
            "p0123": lambda: project_slots((0, 1, 2, 3)),
            "X0": lambda: quantise_x(0),
            "X1": lambda: quantise_x(1),
            "VQ": quantise_v,
            "WQ": lambda: quantise_w(0, 1),
            "WH0": lambda: quantise_w(0, 2),
            "WH1": lambda: quantise_w(1, 2),
            "T0": lambda: retain_half(b, 0, w_mx, v_mx),
            "T1": lambda: retain_half(b, 1, w_mx, v_mx),
            "WV": quantise_wv,
        }
        PLANS = {
            0: "s0 s1 x0 x1 x2 x3 s2 s3 R1 X0 WQ X1",
            1: "s0 s1 x0 x1 x2 x3 s2 s3 p01 p23 X0 VQ WQ X1",
            2: "s0 s1 q0 q1 s2 s3 R0 p01 p23 VQ WQ",
            (3, 2): "s0 s1 s2 s3 p01 p23 R0 VQ WH0 T0 WH1 T1",
            (0, 0): "x0 s0 s1 x1 s2 h1 s3 x2 x3 X0 WV WQ X1",
        }
        for b in range(B):
            for phase, (block, g) in enumerate(BLOCKS):
                gap = (block - g) * K_PASS
                w_grouped = work.tile([P, K_PASS, PACK], BF16, tag="w_grouped", bufs=1, align_bytes=64)
                w_codes = work.tile([P, K_PASS], U32, tag="w_codes", bufs=6, align_bytes=64)
                w_scales = work.tile([P, K_PASS], U8, tag="w_scales", bufs=6, align_bytes=64)
                w_mx[(block, g)] = (w_codes, w_scales)
                if phase < GROUPS:
                    x_words_grouped = work.tile([P, PACK * C], BF16, tag="x_grouped", align_bytes=64)
                    x_codes = work.tile([P, C], U32, tag="x_codes", align_bytes=64)
                    x_scales = work.tile([P, C], U8, tag="x_scales", align_bytes=64)
                    x_grouped[phase] = x_words_grouped
                    x_mx[phase] = (x_codes, x_scales)
                for step in PLANS.get((b, phase), PLANS[phase]).split():
                    STEPS[step]()
            old_v_mx, old_w_mx = v_mx, w_mx
            v_mx, w_mx = {}, {}
            qkT, next_qkT = next_qkT, {}
